import numpy as np
import ml_dtypes


def mxq(x, axis, fmt="e4m3"):
    dtype, down = {"e4m3": (ml_dtypes.float8_e4m3fn, 7), "e5m2": (ml_dtypes.float8_e5m2, 14)}[fmt]
    v = np.moveaxis(np.asarray(x, np.float32).astype(ml_dtypes.bfloat16).astype(np.float64), axis, -1)
    blocks = v.reshape(v.shape[:-1] + (-1, 32))
    amax = np.abs(blocks).max(-1, keepdims=True)
    byte = np.maximum(np.where(amax > 0, np.frexp(amax)[1] - 1 + 127, 0) - down, 1)
    scale = np.exp2(byte - 127.0)
    codes = (blocks / scale).astype(np.float32).astype(dtype).astype(np.float64)
    return np.moveaxis((codes * scale).reshape(v.shape), -1, axis)


WIDE = False


def mx_kscale(k):
    if not WIDE:
        return np.ones(k)
    levels = np.array([10, -10, 5, -5, 0])
    a = np.random.permutation(np.resize(levels, k // 512 * 4)).reshape(k // 512, 4)
    idx = np.arange(k)
    return np.exp2(a[idx // 512, idx % 128 // 32])


BF16 = ml_dtypes.bfloat16


def bf(x):
    return np.asarray(x, np.float32).astype(BF16)


def f64(x):
    return np.asarray(x).astype(np.float64)


E2M1 = np.array([0.0, 0.5, 1.0, 1.5, 2.0, 3.0, 4.0, 6.0, -0.0, -0.5, -1.0, -1.5, -2.0, -3.0, -4.0, -6.0])


def pack_weight(w, fmt):
    k, n = w.shape
    w = f64(bf(w)).reshape(k // 32, 32, n)
    amax = np.abs(w).max(1)
    if fmt == "e4m3":
        byte = np.frexp(amax)[1] - 1 + 127 - 7
    else:
        mant, ex = np.frexp(amax / 6.0)
        byte = np.where(mant > 0.5, ex, ex - 1) + 127
    byte = np.clip(np.where(amax > 0, byte, 1), 1, 254)
    scaled = (w * np.exp2(127.0 - byte)[:, None, :]).reshape(k, n).astype(np.float32)
    by_word = np.ascontiguousarray(scaled.reshape(k // 512, 128, 4, n).transpose(0, 1, 3, 2))
    if fmt == "e4m3":
        words = by_word.astype(ml_dtypes.float8_e4m3fn).view(np.uint8)
    else:
        c = by_word.astype(ml_dtypes.float4_e2m1fn).view(np.uint8) & 0xF
        words = c[..., 0::2] | (c[..., 1::2] << 4)
    return np.ascontiguousarray(words), np.ascontiguousarray(byte.astype(np.uint8).reshape(k // 512, 16, n))


def unpack_weight(words, scales, fmt):
    g, p, n, _ = words.shape
    if fmt == "e4m3":
        vals = np.ascontiguousarray(words).view(ml_dtypes.float8_e4m3fn).astype(np.float64)
    else:
        nib = np.empty((g, p, n, 4), np.uint8)
        nib[..., 0::2] = words & 0xF
        nib[..., 1::2] = words >> 4
        vals = E2M1[nib]
    vals = vals * np.repeat(np.exp2(scales.astype(np.float64) - 127.0), 8, axis=1)[..., None]
    return vals.transpose(0, 1, 3, 2).reshape(g * 512, n)


B, D, L = 8192, 512, 4
FMT = "e4m3"


def relu(v):
    return np.maximum(v, 0.0)


def setup_inputs():
    s = mx_kscale(D)
    h_prev = bf(relu(np.random.standard_normal((B, D))) * s)
    x = bf(np.random.standard_normal((B, D)) * 1.5 / np.sqrt(np.sqrt(D)))
    w_last = np.random.standard_normal((D, D)) * 2.0 / np.sqrt(D) / s[None, :]
    b_last = bf(np.random.standard_normal(D) * 0.2)
    w_out = np.random.standard_normal((D, D)) / np.sqrt(D)
    b_out = bf(np.random.standard_normal(D) * 0.2)
    w_last_words, w_last_scales = pack_weight(np.ascontiguousarray(w_last.T), FMT)
    w_out_words, w_out_scales = pack_weight(np.ascontiguousarray(w_out.T), FMT)
    return {"h_prev": h_prev,
            "x": x,
            "w_last_words": w_last_words,
            "w_last_scales": w_last_scales,
            "b_last": b_last,
            "w_out_words": w_out_words,
            "w_out_scales": w_out_scales,
            "b_out": b_out}


def reference(h_prev, x, w_last_words, w_last_scales, b_last, w_out_words, w_out_scales, b_out):
    xf = f64(x)
    interactions = relu(xf * xf.sum(axis=1, keepdims=True))
    h = relu((mxq(f64(h_prev), 1, "e4m3") @ unpack_weight(w_last_words, w_last_scales, FMT)) + f64(b_last))
    z = (h + interactions) * 0.5
    return (mxq(z, 1, "e4m3") @ unpack_weight(w_out_words, w_out_scales, FMT)) + f64(b_out)

@@ -1,0 +1,191 @@
+from contextlib import ExitStack
+
+import concourse.mybir as mybir
+from concourse.masks import make_identity
+
+F32 = mybir.dt.float32
+BF16 = mybir.dt.bfloat16
+I32 = mybir.dt.int32
+U32 = mybir.dt.uint32
+U8 = mybir.dt.uint8
+FP8X4 = mybir.dt.float8_e4m3fn_x4
+ALU = mybir.AluOpType
+ACT = mybir.ActivationFunctionType
+
+P = 128
+B = 8192
+D = 512
+PACK = 4
+TILES = B // P
+GROUP = 4
+GROUPS = TILES // GROUP
+HALF_WORDS = D // PACK
+
+FLOPS = 2 * 2 * B * D * D
+
+
+def load_weight(nc, consts, words, scales, name):
+    codes = consts.tile([P, D * PACK], U8, name=name + "_codes", align_bytes=64)
+    nc.sync.dma_start(
+        out=codes[:].bitcast(I32),
+        in_=words.rearrange("g p n t -> (g p) (n t)").bitcast(I32),
+    )
+    plane = consts.tile([P, D], U8, name=name + "_scales", align_bytes=64)
+    nc.vector.memset(plane[:].bitcast(I32), 0)
+    for quadrant in range(4):
+        nc.sync.dma_start(
+            out=plane[32 * quadrant : 32 * quadrant + 4, :].bitcast(I32),
+            in_=scales[0, 4 * quadrant : 4 * quadrant + 4, :].bitcast(I32),
+        )
+    return codes, plane
+
+
+def load_bias(nc, consts, bias, factor, name):
+    raw = consts.tile([P, D], BF16, name=name + "_raw")
+    nc.sync.dma_start(out=raw[:], in_=bias.partition_broadcast(P))
+    spread = consts.tile([P, D], F32, name=name)
+    nc.vector.tensor_scalar(out=spread[:], in0=raw[:], scalar1=factor, scalar2=None, op0=ALU.mult)
+    return spread
+
+
+def tile_deepfm_pa_t_kernel(
+    tc, h_prev, x, w_last_words, w_last_scales, b_last, w_out_words, w_out_scales, b_out, out
+):
+    nc = tc.nc
+    h_rows = h_prev.rearrange("(p t) d -> p t d", t=TILES)
+    x_rows = x.rearrange("(p t) d -> p t d", t=TILES)
+    out_rows = out.rearrange("(p t) d -> p t d", t=TILES)
+
+    with ExitStack() as stack:
+        consts = stack.enter_context(tc.tile_pool(name="consts", bufs=1))
+        inputs = stack.enter_context(tc.tile_pool(name="inputs", bufs=1))
+        work = stack.enter_context(tc.tile_pool(name="work", bufs=2))
+        sums = stack.enter_context(tc.tile_pool(name="sums", bufs=3))
+        flipped = stack.enter_context(tc.psum_pool(name="flipped", bufs=4))
+        banks = stack.enter_context(tc.psum_pool(name="banks", bufs=4))
+
+        h_in, x_in = [], []
+
+        def load_group(g):
+            rows = slice(g * GROUP, (g + 1) * GROUP)
+            h_in.append(inputs.tile([P, GROUP, D], BF16, name="h%d" % g))
+            nc.sync.dma_start(out=h_in[g][:], in_=h_rows[:, rows, :])
+            x_in.append(inputs.tile([P, GROUP, D], BF16, name="x%d" % g))
+            nc.sync.dma_start(out=x_in[g][:], in_=x_rows[:, rows, :])
+
+        w1_codes, w1_scales = load_weight(nc, consts, w_last_words, w_last_scales, "w1")
+        load_group(0)
+        half_b1 = load_bias(nc, consts, b_last, 0.5, "half_b1")
+        w2_codes, w2_scales = load_weight(nc, consts, w_out_words, w_out_scales, "w2")
+        b2 = load_bias(nc, consts, b_out, 1.0, "b2")
+        for g in range(1, GROUPS):
+            load_group(g)
+
+        identity = consts.tile([P, P], F32, name="identity")
+        make_identity(nc, identity[:])
+        half_rowsum = consts.tile([P, TILES], F32, name="half_rowsum")
+        unread = consts.tile([P, GROUP, D], BF16, name="unread")
+
+        fm, z_rows, grouped, codes, planes, acc1, acc2 = {}, {}, {}, {}, {}, {}, {}
+
+        def fm_term(g):
+            fm[g] = work.tile([P, GROUP, D], F32, name="fm")
+            for j in range(GROUP):
+                nc.scalar.activation(
+                    out=unread[:, j, :],
+                    in_=x_in[g][:, j, :],
+                    func=ACT.Copy,
+                    scale=0.5,
+                    accum_out=half_rowsum[:, g * GROUP + j : g * GROUP + j + 1],
+                )
+            for j in range(GROUP):
+                nc.scalar.activation(
+                    out=fm[g][:, j, :],
+                    in_=x_in[g][:, j, :],
+                    func=ACT.Relu,
+                    scale=half_rowsum[:, g * GROUP + j : g * GROUP + j + 1],
+                )
+
+        def transpose(rows, key):
+            grouped[key] = work.tile([P, GROUP * D], BF16, name="grouped_" + key[0], align_bytes=64)
+            pairs = grouped[key][:].bitcast(F32).rearrange("p (j r u) -> p j r u", j=GROUP, u=2)
+            for first in range(0, GROUP, 2):
+                bank = flipped.tile([P, 2, 2, P], F32, name="bank")
+                for j in range(2):
+                    words = rows[:, first + j, :].bitcast(F32)
+                    for u in range(2):
+                        nc.tensor.transpose(bank[:, j, u, :], words[:, u : 2 * HALF_WORDS : 2], identity[:])
+                nc.scalar.copy(
+                    out=pairs[:, first : first + 2, :, :],
+                    in_=bank[:].rearrange("p j u r -> p j r u"),
+                )
+
+        def quantise(key):
+            codes[key] = work.tile([P, GROUP * P], U32, name="codes_" + key[0], align_bytes=64)
+            planes[key] = work.tile([P, GROUP * P], U8, name="planes_" + key[0], align_bytes=64)
+            nc.vector.quantize_mx(
+                out=codes[key][:].bitcast(FP8X4), scales=planes[key][:], in_=grouped[key][:]
+            )
+
+        def mx_pass(key, j, w_codes, w_scales):
+            acc = banks.tile([P, D], F32, name="acc")
+            cols = slice(j * P, (j + 1) * P)
+            nc.tensor.matmul_mx(
+                out=acc[:],
+                lhsT=codes[key][:, cols].bitcast(FP8X4),
+                lhsT_scale=planes[key][:, cols],
+                rhs=w_codes[:].bitcast(FP8X4),
+                rhs_scale=w_scales[:],
+                start=True,
+                stop=True,
+            )
+            return acc
+
+        def in_range(g):
+            return 0 <= g < GROUPS
+
+        stack.enter_context(tc.manual_schedule())
+        for k in range(-2, GROUPS + 2):
+            if in_range(k + 1):
+                fm_term(k + 1)
+
+            if in_range(k):
+                z_rows[k] = work.tile([P, GROUP, D], BF16, name="z_rows")
+            pre = {}
+            for j in range(GROUP + 1):
+                if in_range(k) and j < GROUP:
+                    pre[j] = sums.tile([P, D], F32, name="pre")
+                    nc.vector.scalar_tensor_tensor(
+                        out=pre[j][:], in0=acc1[k, j][:], scalar=0.5, in1=half_b1[:], op0=ALU.mult, op1=ALU.add
+                    )
+                if in_range(k - 2) and j < GROUP:
+                    acc2[k - 2, j] = mx_pass(("z", k - 2), j, w2_codes, w2_scales)
+                if in_range(k) and j > 0:
+                    nc.vector.scalar_tensor_tensor(
+                        out=z_rows[k][:, j - 1, :],
+                        in0=pre[j - 1][:],
+                        scalar=0.0,
+                        in1=fm[k][:, j - 1, :],
+                        op0=ALU.max,
+                        op1=ALU.add,
+                    )
+
+            if in_range(k + 1):
+                quantise(("h", k + 1))
+            if in_range(k - 1):
+                quantise(("z", k - 1))
+
+            if in_range(k + 2):
+                transpose(h_in[k + 2], ("h", k + 2))
+            if in_range(k):
+                transpose(z_rows[k], ("z", k))
+
+            if in_range(k - 2):
+                result = sums.tile([P, GROUP, D], F32, name="result")
+            for j in range(GROUP):
+                if in_range(k - 2):
+                    nc.vector.tensor_tensor(out=result[:, j, :], in0=acc2[k - 2, j][:], in1=b2[:], op=ALU.add)
+                if in_range(k + 1):
+                    acc1[k + 1, j] = mx_pass(("h", k + 1), j, w1_codes, w1_scales)
+            if in_range(k - 2):
+                nc.sync.dma_start(out=out_rows[:, (k - 2) * GROUP : (k - 1) * GROUP, :], in_=result[:])

@@ -20,6 +20,8 @@ TILES = B // P
 GROUP = 4
 GROUPS = TILES // GROUP
 HALF_WORDS = D // PACK
+FIRST_LOADS = 3
+INPUT_BUFS = 6
 
 FLOPS = 2 * 2 * B * D * D
 
@@ -58,19 +60,19 @@ def tile_deepfm_pa_t_kernel(
 
     with ExitStack() as stack:
         consts = stack.enter_context(tc.tile_pool(name="consts", bufs=1))
-        inputs = stack.enter_context(tc.tile_pool(name="inputs", bufs=1))
+        inputs = stack.enter_context(tc.tile_pool(name="inputs", bufs=INPUT_BUFS))
         work = stack.enter_context(tc.tile_pool(name="work", bufs=2))
-        sums = stack.enter_context(tc.tile_pool(name="sums", bufs=3))
+        slack = stack.enter_context(tc.tile_pool(name="slack", bufs=3))
         flipped = stack.enter_context(tc.psum_pool(name="flipped", bufs=4))
         banks = stack.enter_context(tc.psum_pool(name="banks", bufs=4))
 
-        h_in, x_in = [], []
+        h_in, x_in = {}, {}
 
         def load_group(g):
             rows = slice(g * GROUP, (g + 1) * GROUP)
-            h_in.append(inputs.tile([P, GROUP, D], BF16, name="h%d" % g))
+            h_in[g] = inputs.tile([P, GROUP, D], BF16, name="h_in")
             nc.sync.dma_start(out=h_in[g][:], in_=h_rows[:, rows, :])
-            x_in.append(inputs.tile([P, GROUP, D], BF16, name="x%d" % g))
+            x_in[g] = inputs.tile([P, GROUP, D], BF16, name="x_in")
             nc.sync.dma_start(out=x_in[g][:], in_=x_rows[:, rows, :])
 
         w1_codes, w1_scales = load_weight(nc, consts, w_last_words, w_last_scales, "w1")
@@ -78,7 +80,7 @@ def tile_deepfm_pa_t_kernel(
         half_b1 = load_bias(nc, consts, b_last, 0.5, "half_b1")
         w2_codes, w2_scales = load_weight(nc, consts, w_out_words, w_out_scales, "w2")
         b2 = load_bias(nc, consts, b_out, 1.0, "b2")
-        for g in range(1, GROUPS):
+        for g in range(1, FIRST_LOADS):
             load_group(g)
 
         identity = consts.tile([P, P], F32, name="identity")
@@ -86,10 +88,10 @@ def tile_deepfm_pa_t_kernel(
         half_rowsum = consts.tile([P, TILES], F32, name="half_rowsum")
         unread = consts.tile([P, GROUP, D], BF16, name="unread")
 
-        fm, z_rows, grouped, codes, planes, acc1, acc2 = {}, {}, {}, {}, {}, {}, {}
+        fm, deep, z_rows, grouped, codes, planes, acc1, acc2 = {}, {}, {}, {}, {}, {}, {}, {}
 
         def fm_term(g):
-            fm[g] = work.tile([P, GROUP, D], F32, name="fm")
+            fm[g] = slack.tile([P, GROUP, D], F32, name="fm")
             for j in range(GROUP):
                 nc.scalar.activation(
                     out=unread[:, j, :],
@@ -145,47 +147,46 @@ def tile_deepfm_pa_t_kernel(
             return 0 <= g < GROUPS
 
         stack.enter_context(tc.manual_schedule())
-        for k in range(-2, GROUPS + 2):
+        for k in range(-2, GROUPS + 3):
+            if in_range(k + 2 + FIRST_LOADS):
+                load_group(k + 2 + FIRST_LOADS)
             if in_range(k + 1):
                 fm_term(k + 1)
 
             if in_range(k):
-                z_rows[k] = work.tile([P, GROUP, D], BF16, name="z_rows")
-            pre = {}
-            for j in range(GROUP + 1):
-                if in_range(k) and j < GROUP:
-                    pre[j] = sums.tile([P, D], F32, name="pre")
+                deep[k] = work.tile([P, GROUP, D], F32, name="deep")
+            for j in range(GROUP):
+                if in_range(k):
                     nc.vector.scalar_tensor_tensor(
-                        out=pre[j][:], in0=acc1[k, j][:], scalar=0.5, in1=half_b1[:], op0=ALU.mult, op1=ALU.add
+                        out=deep[k][:, j, :], in0=acc1[k, j][:], scalar=0.5, in1=half_b1[:], op0=ALU.mult, op1=ALU.add
                     )
-                if in_range(k - 2) and j < GROUP:
-                    acc2[k - 2, j] = mx_pass(("z", k - 2), j, w2_codes, w2_scales)
-                if in_range(k) and j > 0:
-                    nc.vector.scalar_tensor_tensor(
-                        out=z_rows[k][:, j - 1, :],
-                        in0=pre[j - 1][:],
-                        scalar=0.0,
-                        in1=fm[k][:, j - 1, :],
-                        op0=ALU.max,
-                        op1=ALU.add,
-                    )
+                if in_range(k - 3):
+                    acc2[k - 3, j] = mx_pass(("z", k - 3), j, w2_codes, w2_scales)
 
             if in_range(k + 1):
                 quantise(("h", k + 1))
-            if in_range(k - 1):
-                quantise(("z", k - 1))
+            if in_range(k):
+                nc.vector.tensor_scalar_max(out=deep[k][:], in0=deep[k][:], scalar1=0.0)
+            if in_range(k - 2):
+                quantise(("z", k - 2))
+            if in_range(k):
+                z_rows[k] = work.tile([P, GROUP, D], BF16, name="z_rows")
+                for j in range(GROUP):
+                    nc.gpsimd.tensor_tensor(
+                        out=z_rows[k][:, j, :], in0=deep[k][:, j, :], in1=fm[k][:, j, :], op=ALU.add
+                    )
 
             if in_range(k + 2):
                 transpose(h_in[k + 2], ("h", k + 2))
-            if in_range(k):
-                transpose(z_rows[k], ("z", k))
+            if in_range(k - 1):
+                transpose(z_rows[k - 1], ("z", k - 1))
 
-            if in_range(k - 2):
-                result = sums.tile([P, GROUP, D], F32, name="result")
+            if in_range(k - 3):
+                result = slack.tile([P, GROUP, D], F32, name="result")
             for j in range(GROUP):
-                if in_range(k - 2):
-                    nc.vector.tensor_tensor(out=result[:, j, :], in0=acc2[k - 2, j][:], in1=b2[:], op=ALU.add)
+                if in_range(k - 3):
+                    nc.vector.tensor_tensor(out=result[:, j, :], in0=acc2[k - 3, j][:], in1=b2[:], op=ALU.add)
                 if in_range(k + 1):
                     acc1[k + 1, j] = mx_pass(("h", k + 1), j, w1_codes, w1_scales)
-            if in_range(k - 2):
-                nc.sync.dma_start(out=out_rows[:, (k - 2) * GROUP : (k - 1) * GROUP, :], in_=result[:])
+            if in_range(k - 3):
+                nc.sync.dma_start(out=out_rows[:, (k - 3) * GROUP : (k - 2) * GROUP, :], in_=result[:])

@@ -21,6 +21,7 @@ GROUP = 4
 GROUPS = TILES // GROUP
 HALF_WORDS = D // PACK
 FIRST_LOADS = 3
+GPSIMD_TILES = 3
 INPUT_BUFS = 6
 
 FLOPS = 2 * 2 * B * D * D
@@ -166,12 +167,23 @@ def tile_deepfm_pa_t_kernel(
             if in_range(k + 1):
                 quantise(("h", k + 1))
             if in_range(k):
-                nc.vector.tensor_scalar_max(out=deep[k][:], in0=deep[k][:], scalar1=0.0)
+                z_rows[k] = work.tile([P, GROUP, D], BF16, name="z_rows")
+                nc.vector.tensor_scalar_max(
+                    out=deep[k][:, :GPSIMD_TILES, :], in0=deep[k][:, :GPSIMD_TILES, :], scalar1=0.0
+                )
+                for j in range(GPSIMD_TILES, GROUP):
+                    nc.vector.scalar_tensor_tensor(
+                        out=z_rows[k][:, j, :],
+                        in0=deep[k][:, j, :],
+                        scalar=0.0,
+                        in1=fm[k][:, j, :],
+                        op0=ALU.max,
+                        op1=ALU.add,
+                    )
             if in_range(k - 2):
                 quantise(("z", k - 2))
             if in_range(k):
-                z_rows[k] = work.tile([P, GROUP, D], BF16, name="z_rows")
-                for j in range(GROUP):
+                for j in range(GPSIMD_TILES):
                     nc.gpsimd.tensor_tensor(
                         out=z_rows[k][:, j, :], in0=deep[k][:, j, :], in1=fm[k][:, j, :], op=ALU.add
                     )

@@ -21,7 +21,7 @@ GROUP = 4
 GROUPS = TILES // GROUP
 HALF_WORDS = D // PACK
 FIRST_LOADS = 3
-GPSIMD_TILES = 3
+VECTOR_TILES = 2
 INPUT_BUFS = 6
 
 FLOPS = 2 * 2 * B * D * D
@@ -168,10 +168,7 @@ def tile_deepfm_pa_t_kernel(
                 quantise(("h", k + 1))
             if in_range(k):
                 z_rows[k] = work.tile([P, GROUP, D], BF16, name="z_rows")
-                nc.vector.tensor_scalar_max(
-                    out=deep[k][:, :GPSIMD_TILES, :], in0=deep[k][:, :GPSIMD_TILES, :], scalar1=0.0
-                )
-                for j in range(GPSIMD_TILES, GROUP):
+                for j in range(VECTOR_TILES):
                     nc.vector.scalar_tensor_tensor(
                         out=z_rows[k][:, j, :],
                         in0=deep[k][:, j, :],
@@ -183,7 +180,15 @@ def tile_deepfm_pa_t_kernel(
             if in_range(k - 2):
                 quantise(("z", k - 2))
             if in_range(k):
-                for j in range(GPSIMD_TILES):
+                nc.gpsimd.tensor_scalar(
+                    out=deep[k][:, VECTOR_TILES:, :],
+                    in0=deep[k][:, VECTOR_TILES:, :],
+                    scalar1=0.0,
+                    scalar2=0.0,
+                    op0=ALU.max,
+                    op1=ALU.add,
+                )
+                for j in range(VECTOR_TILES, GROUP):
                     nc.gpsimd.tensor_tensor(
                         out=z_rows[k][:, j, :], in0=deep[k][:, j, :], in1=fm[k][:, j, :], op=ALU.add
                     )

@@ -21,7 +21,7 @@ GROUP = 4
 GROUPS = TILES // GROUP
 HALF_WORDS = D // PACK
 FIRST_LOADS = 3
-VECTOR_TILES = 2
+GPSIMD_TILES = 3
 INPUT_BUFS = 6
 
 FLOPS = 2 * 2 * B * D * D
@@ -76,8 +76,8 @@ def tile_deepfm_pa_t_kernel(
             x_in[g] = inputs.tile([P, GROUP, D], BF16, name="x_in")
             nc.sync.dma_start(out=x_in[g][:], in_=x_rows[:, rows, :])
 
-        w1_codes, w1_scales = load_weight(nc, consts, w_last_words, w_last_scales, "w1")
         load_group(0)
+        w1_codes, w1_scales = load_weight(nc, consts, w_last_words, w_last_scales, "w1")
         half_b1 = load_bias(nc, consts, b_last, 0.5, "half_b1")
         w2_codes, w2_scales = load_weight(nc, consts, w_out_words, w_out_scales, "w2")
         b2 = load_bias(nc, consts, b_out, 1.0, "b2")
@@ -168,7 +168,10 @@ def tile_deepfm_pa_t_kernel(
                 quantise(("h", k + 1))
             if in_range(k):
                 z_rows[k] = work.tile([P, GROUP, D], BF16, name="z_rows")
-                for j in range(VECTOR_TILES):
+                nc.vector.tensor_scalar_max(
+                    out=deep[k][:, :GPSIMD_TILES, :], in0=deep[k][:, :GPSIMD_TILES, :], scalar1=0.0
+                )
+                for j in range(GPSIMD_TILES, GROUP):
                     nc.vector.scalar_tensor_tensor(
                         out=z_rows[k][:, j, :],
                         in0=deep[k][:, j, :],
@@ -180,15 +183,7 @@ def tile_deepfm_pa_t_kernel(
             if in_range(k - 2):
                 quantise(("z", k - 2))
             if in_range(k):
-                nc.gpsimd.tensor_scalar(
-                    out=deep[k][:, VECTOR_TILES:, :],
-                    in0=deep[k][:, VECTOR_TILES:, :],
-                    scalar1=0.0,
-                    scalar2=0.0,
-                    op0=ALU.max,
-                    op1=ALU.add,
-                )
-                for j in range(VECTOR_TILES, GROUP):
+                for j in range(GPSIMD_TILES):
                     nc.gpsimd.tensor_tensor(
                         out=z_rows[k][:, j, :], in0=deep[k][:, j, :], in1=fm[k][:, j, :], op=ALU.add
                     )
@@ -203,7 +198,6 @@ def tile_deepfm_pa_t_kernel(
             for j in range(GROUP):
                 if in_range(k - 3):
                     nc.vector.tensor_tensor(out=result[:, j, :], in0=acc2[k - 3, j][:], in1=b2[:], op=ALU.add)
+                    nc.sync.dma_start(out=out_rows[:, (k - 3) * GROUP + j, :], in_=result[:, j, :])
                 if in_range(k + 1):
                     acc1[k + 1, j] = mx_pass(("h", k + 1), j, w1_codes, w1_scales)
-            if in_range(k - 3):
-                nc.sync.dma_start(out=out_rows[:, (k - 3) * GROUP : (k - 2) * GROUP, :], in_=result[:])

@@ -19,9 +19,7 @@ PACK = 4
 TILES = B // P
 GROUP = 4
 GROUPS = TILES // GROUP
-HALF_WORDS = D // PACK
 FIRST_LOADS = 3
-GPSIMD_TILES = 3
 INPUT_BUFS = 6
 
 FLOPS = 2 * 2 * B * D * D
@@ -43,14 +41,6 @@ def load_weight(nc, consts, words, scales, name):
     return codes, plane
 
 
-def load_bias(nc, consts, bias, factor, name):
-    raw = consts.tile([P, D], BF16, name=name + "_raw")
-    nc.sync.dma_start(out=raw[:], in_=bias.partition_broadcast(P))
-    spread = consts.tile([P, D], F32, name=name)
-    nc.vector.tensor_scalar(out=spread[:], in0=raw[:], scalar1=factor, scalar2=None, op0=ALU.mult)
-    return spread
-
-
 def tile_deepfm_pa_t_kernel(
     tc, h_prev, x, w_last_words, w_last_scales, b_last, w_out_words, w_out_scales, b_out, out
 ):
@@ -64,8 +54,7 @@ def tile_deepfm_pa_t_kernel(
         inputs = stack.enter_context(tc.tile_pool(name="inputs", bufs=INPUT_BUFS))
         work = stack.enter_context(tc.tile_pool(name="work", bufs=2))
         slack = stack.enter_context(tc.tile_pool(name="slack", bufs=3))
-        flipped = stack.enter_context(tc.psum_pool(name="flipped", bufs=4))
-        banks = stack.enter_context(tc.psum_pool(name="banks", bufs=4))
+        banks = stack.enter_context(tc.psum_pool(name="banks", bufs=2))
 
         h_in, x_in = {}, {}
 
@@ -78,50 +67,79 @@ def tile_deepfm_pa_t_kernel(
 
         load_group(0)
         w1_codes, w1_scales = load_weight(nc, consts, w_last_words, w_last_scales, "w1")
-        half_b1 = load_bias(nc, consts, b_last, 0.5, "half_b1")
+        b1_raw = consts.tile([P, PACK], BF16, name="b1_raw")
+        nc.sync.dma_start(out=b1_raw[:], in_=b_last.rearrange("(p t) -> p t", t=PACK))
         w2_codes, w2_scales = load_weight(nc, consts, w_out_words, w_out_scales, "w2")
-        b2 = load_bias(nc, consts, b_out, 1.0, "b2")
+        b2_raw = consts.tile([P, D], BF16, name="b2_raw")
+        nc.sync.dma_start(out=b2_raw[:], in_=b_out.partition_broadcast(P))
         for g in range(1, FIRST_LOADS):
             load_group(g)
 
         identity = consts.tile([P, P], F32, name="identity")
         make_identity(nc, identity[:])
+
+        w1_by_pass = consts.tile([P, D * PACK], U8, name="w1_by_pass", align_bytes=64)
+        nc.vector.tensor_copy(
+            out=w1_by_pass[:].bitcast(I32).rearrange("p (t m) -> p t m", t=PACK),
+            in_=w1_codes[:].bitcast(I32).rearrange("p (m t) -> p t m", t=PACK),
+        )
+        w1_scales_by_pass = consts.tile([P, D], U8, name="w1_scales_by_pass", align_bytes=64)
+        nc.vector.tensor_copy(
+            out=w1_scales_by_pass[:].rearrange("p (t m) -> p t m", t=PACK),
+            in_=w1_scales[:].rearrange("p (m t) -> p t m", t=PACK),
+        )
+        half_b1 = consts.tile([P, PACK], F32, name="half_b1")
+        nc.vector.tensor_scalar(out=half_b1[:], in0=b1_raw[:], scalar1=0.5, scalar2=None, op0=ALU.mult)
+        b2 = consts.tile([P, D], F32, name="b2")
+        nc.vector.tensor_copy(out=b2[:], in_=b2_raw[:])
+
         half_rowsum = consts.tile([P, TILES], F32, name="half_rowsum")
         unread = consts.tile([P, GROUP, D], BF16, name="unread")
 
-        fm, deep, z_rows, grouped, codes, planes, acc1, acc2 = {}, {}, {}, {}, {}, {}, {}, {}
+        fm, deep, grouped, codes, planes = {}, {}, {}, {}, {}
+        h_bank, fm_bank, acc1, acc2, result = {}, {}, {}, {}, {}
 
-        def fm_term(g):
-            fm[g] = slack.tile([P, GROUP, D], F32, name="fm")
-            for j in range(GROUP):
-                nc.scalar.activation(
-                    out=unread[:, j, :],
-                    in_=x_in[g][:, j, :],
-                    func=ACT.Copy,
-                    scale=0.5,
-                    accum_out=half_rowsum[:, g * GROUP + j : g * GROUP + j + 1],
-                )
-            for j in range(GROUP):
-                nc.scalar.activation(
-                    out=fm[g][:, j, :],
-                    in_=x_in[g][:, j, :],
-                    func=ACT.Relu,
-                    scale=half_rowsum[:, g * GROUP + j : g * GROUP + j + 1],
-                )
+        def row_sum(g, j):
+            nc.scalar.activation(
+                out=unread[:, j, :],
+                in_=x_in[g][:, j, :],
+                func=ACT.Copy,
+                scale=0.5,
+                accum_out=half_rowsum[:, g * GROUP + j : g * GROUP + j + 1],
+            )
 
-        def transpose(rows, key):
-            grouped[key] = work.tile([P, GROUP * D], BF16, name="grouped_" + key[0], align_bytes=64)
-            pairs = grouped[key][:].bitcast(F32).rearrange("p (j r u) -> p j r u", j=GROUP, u=2)
-            for first in range(0, GROUP, 2):
-                bank = flipped.tile([P, 2, 2, P], F32, name="bank")
-                for j in range(2):
-                    words = rows[:, first + j, :].bitcast(F32)
-                    for u in range(2):
-                        nc.tensor.transpose(bank[:, j, u, :], words[:, u : 2 * HALF_WORDS : 2], identity[:])
-                nc.scalar.copy(
-                    out=pairs[:, first : first + 2, :, :],
-                    in_=bank[:].rearrange("p j u r -> p j r u"),
-                )
+        def fm_product(g, j):
+            if j == 0:
+                fm[g] = work.tile([P, GROUP, PACK, P], F32, name="fm")
+            nc.gpsimd.tensor_scalar(
+                out=fm[g][:, j, :, :],
+                in0=x_in[g][:, j, :].rearrange("p (q t) -> p t q", t=PACK),
+                scalar1=half_rowsum[:, g * GROUP + j : g * GROUP + j + 1],
+                scalar2=0.0,
+                op0=ALU.mult,
+                op1=ALU.add,
+            )
+
+        def flip_fm(g, j):
+            fm_bank[g, j] = banks.tile([P, PACK, P], F32, name="fm_bank")
+            for t in range(PACK):
+                nc.tensor.transpose(fm_bank[g, j][:, t, :], fm[g][:, j, t, :], identity[:])
+
+        def flip_h(g, pair):
+            h_bank[g, pair] = banks.tile([P, 2, 2, P], F32, name="h_bank")
+            for j in range(2):
+                words = h_in[g][:, 2 * pair + j, :].bitcast(F32)
+                for u in range(2):
+                    nc.tensor.transpose(h_bank[g, pair][:, j, u, :], words[:, u::2], identity[:])
+
+        def copy_h(g, pair):
+            if pair == 0:
+                grouped["h", g] = work.tile([P, GROUP * D], BF16, name="grouped_h", align_bytes=64)
+            pairs = grouped["h", g][:].bitcast(F32).rearrange("p (j r u) -> p j r u", j=GROUP, u=2)
+            nc.scalar.copy(
+                out=pairs[:, 2 * pair : 2 * pair + 2, :, :],
+                in_=h_bank[g, pair][:].rearrange("p j u r -> p j r u"),
+            )
 
         def quantise(key):
             codes[key] = work.tile([P, GROUP * P], U32, name="codes_" + key[0], align_bytes=64)
@@ -130,74 +148,98 @@ def tile_deepfm_pa_t_kernel(
                 out=codes[key][:].bitcast(FP8X4), scales=planes[key][:], in_=grouped[key][:]
             )
 
-        def mx_pass(key, j, w_codes, w_scales):
-            acc = banks.tile([P, D], F32, name="acc")
-            cols = slice(j * P, (j + 1) * P)
+        def layer1(g, t):
+            acc1[g, t] = banks.tile([P, GROUP * P], F32, name="acc1")
+            cols = slice(t * P, (t + 1) * P)
             nc.tensor.matmul_mx(
-                out=acc[:],
-                lhsT=codes[key][:, cols].bitcast(FP8X4),
-                lhsT_scale=planes[key][:, cols],
-                rhs=w_codes[:].bitcast(FP8X4),
-                rhs_scale=w_scales[:],
+                out=acc1[g, t][:],
+                lhsT=w1_by_pass[:].bitcast(U32)[:, cols].bitcast(FP8X4),
+                lhsT_scale=w1_scales_by_pass[:, cols],
+                rhs=codes["h", g][:].bitcast(FP8X4),
+                rhs_scale=planes["h", g][:],
                 start=True,
                 stop=True,
             )
-            return acc
+
+        def leave_layer1(g, t):
+            if t == 0:
+                deep[g] = work.tile([P, PACK, GROUP * P], F32, name="deep")
+            nc.scalar.activation(
+                out=deep[g][:, t, :], in_=acc1[g, t][:], func=ACT.Relu, scale=0.5, bias=half_b1[:, t : t + 1]
+            )
+
+        def make_z(g, j):
+            if j == 0:
+                grouped["z", g] = work.tile([P, GROUP * D], BF16, name="grouped_z", align_bytes=64)
+            z = grouped["z", g][:].rearrange("p (j r t) -> p j r t", j=GROUP, t=PACK)
+            nc.vector.scalar_tensor_tensor(
+                out=z[:, j, :, :],
+                in0=fm_bank[g, j][:].rearrange("p t r -> p r t"),
+                scalar=0.0,
+                in1=deep[g][:, :, j * P : (j + 1) * P].rearrange("p t r -> p r t"),
+                op0=ALU.max,
+                op1=ALU.add,
+            )
+
+        def layer2(g, j):
+            acc2[g, j] = banks.tile([P, D], F32, name="acc2")
+            cols = slice(j * P, (j + 1) * P)
+            nc.tensor.matmul_mx(
+                out=acc2[g, j][:],
+                lhsT=codes["z", g][:, cols].bitcast(FP8X4),
+                lhsT_scale=planes["z", g][:, cols],
+                rhs=w2_codes[:].bitcast(FP8X4),
+                rhs_scale=w2_scales[:],
+                start=True,
+                stop=True,
+            )
+
+        def leave_layer2(g, j):
+            if j == 0:
+                result[g] = slack.tile([P, GROUP, D], F32, name="result")
+            nc.vector.tensor_tensor(out=result[g][:, j, :], in0=acc2[g, j][:], in1=b2[:], op=ALU.add)
+            nc.sync.dma_start(out=out_rows[:, g * GROUP + j, :], in_=result[g][:, j, :])
 
         def in_range(g):
             return 0 <= g < GROUPS
 
         stack.enter_context(tc.manual_schedule())
-        for k in range(-2, GROUPS + 3):
+        for k in range(-2, GROUPS + 1):
             if in_range(k + 2 + FIRST_LOADS):
                 load_group(k + 2 + FIRST_LOADS)
-            if in_range(k + 1):
-                fm_term(k + 1)
-
-            if in_range(k):
-                deep[k] = work.tile([P, GROUP, D], F32, name="deep")
-            for j in range(GROUP):
-                if in_range(k):
-                    nc.vector.scalar_tensor_tensor(
-                        out=deep[k][:, j, :], in0=acc1[k, j][:], scalar=0.5, in1=half_b1[:], op0=ALU.mult, op1=ALU.add
-                    )
-                if in_range(k - 3):
-                    acc2[k - 3, j] = mx_pass(("z", k - 3), j, w2_codes, w2_scales)
 
             if in_range(k + 1):
                 quantise(("h", k + 1))
-            if in_range(k):
-                z_rows[k] = work.tile([P, GROUP, D], BF16, name="z_rows")
-                nc.vector.tensor_scalar_max(
-                    out=deep[k][:, :GPSIMD_TILES, :], in0=deep[k][:, :GPSIMD_TILES, :], scalar1=0.0
-                )
-                for j in range(GPSIMD_TILES, GROUP):
-                    nc.vector.scalar_tensor_tensor(
-                        out=z_rows[k][:, j, :],
-                        in0=deep[k][:, j, :],
-                        scalar=0.0,
-                        in1=fm[k][:, j, :],
-                        op0=ALU.max,
-                        op1=ALU.add,
-                    )
-            if in_range(k - 2):
-                quantise(("z", k - 2))
-            if in_range(k):
-                for j in range(GPSIMD_TILES):
-                    nc.gpsimd.tensor_tensor(
-                        out=z_rows[k][:, j, :], in0=deep[k][:, j, :], in1=fm[k][:, j, :], op=ALU.add
-                    )
-
-            if in_range(k + 2):
-                transpose(h_in[k + 2], ("h", k + 2))
             if in_range(k - 1):
-                transpose(z_rows[k - 1], ("z", k - 1))
-
-            if in_range(k - 3):
-                result = slack.tile([P, GROUP, D], F32, name="result")
-            for j in range(GROUP):
-                if in_range(k - 3):
-                    nc.vector.tensor_tensor(out=result[:, j, :], in0=acc2[k - 3, j][:], in1=b2[:], op=ALU.add)
-                    nc.sync.dma_start(out=out_rows[:, (k - 3) * GROUP + j, :], in_=result[:, j, :])
+                quantise(("z", k - 1))
+            for half in range(2):
+                pair = (2 * half, 2 * half + 1)
+                if in_range(k):
+                    for j in pair:
+                        flip_fm(k, j)
+                if in_range(k + 2) and half == 0:
+                    flip_h(k + 2, 0)
+                    flip_h(k + 2, 1)
+                    copy_h(k + 2, 0)
+                    copy_h(k + 2, 1)
                 if in_range(k + 1):
-                    acc1[k + 1, j] = mx_pass(("h", k + 1), j, w1_codes, w1_scales)
+                    for t in pair:
+                        layer1(k + 1, t)
+                if in_range(k - 1):
+                    for j in pair:
+                        layer2(k - 1, j)
+                if in_range(k + 1):
+                    if half == 1:
+                        for j in range(GROUP):
+                            row_sum(k + 1, j)
+                    for t in pair:
+                        leave_layer1(k + 1, t)
+                if in_range(k):
+                    for j in pair:
+                        make_z(k, j)
+                if in_range(k - 1):
+                    for j in pair:
+                        leave_layer2(k - 1, j)
+                if in_range(k + 1) and half == 1:
+                    for j in range(GROUP):
+                        fm_product(k + 1, j)

@@ -19,8 +19,9 @@ PACK = 4
 TILES = B // P
 GROUP = 4
 GROUPS = TILES // GROUP
-FIRST_LOADS = 3
+FIRST_LOADS = 4
 INPUT_BUFS = 6
+VECTOR_SUM_GROUPS = 2
 
 FLOPS = 2 * 2 * B * D * D
 
@@ -69,35 +70,38 @@ def tile_deepfm_pa_t_kernel(
         w1_codes, w1_scales = load_weight(nc, consts, w_last_words, w_last_scales, "w1")
         b1_raw = consts.tile([P, PACK], BF16, name="b1_raw")
         nc.sync.dma_start(out=b1_raw[:], in_=b_last.rearrange("(p t) -> p t", t=PACK))
+        b2_row = consts.tile([P, D], BF16, name="b2_row")
+        nc.vector.memset(b2_row[:], 0.0)
+        nc.sync.dma_start(out=b2_row[:1, :], in_=b_out.rearrange("(o d) -> o d", o=1))
+        load_group(1)
+        load_group(2)
         w2_codes, w2_scales = load_weight(nc, consts, w_out_words, w_out_scales, "w2")
-        b2_raw = consts.tile([P, D], BF16, name="b2_raw")
-        nc.sync.dma_start(out=b2_raw[:], in_=b_out.partition_broadcast(P))
-        for g in range(1, FIRST_LOADS):
-            load_group(g)
+        load_group(3)
 
         identity = consts.tile([P, P], F32, name="identity")
         make_identity(nc, identity[:])
-
+        ones = consts.tile([P, P], BF16, name="ones")
+        nc.gpsimd.memset(ones[:], 1.0)
         w1_by_pass = consts.tile([P, D * PACK], U8, name="w1_by_pass", align_bytes=64)
-        nc.vector.tensor_copy(
-            out=w1_by_pass[:].bitcast(I32).rearrange("p (t m) -> p t m", t=PACK),
-            in_=w1_codes[:].bitcast(I32).rearrange("p (m t) -> p t m", t=PACK),
-        )
         w1_scales_by_pass = consts.tile([P, D], U8, name="w1_scales_by_pass", align_bytes=64)
-        nc.vector.tensor_copy(
-            out=w1_scales_by_pass[:].rearrange("p (t m) -> p t m", t=PACK),
-            in_=w1_scales[:].rearrange("p (m t) -> p t m", t=PACK),
-        )
         half_b1 = consts.tile([P, PACK], F32, name="half_b1")
-        nc.vector.tensor_scalar(out=half_b1[:], in0=b1_raw[:], scalar1=0.5, scalar2=None, op0=ALU.mult)
         b2 = consts.tile([P, D], F32, name="b2")
-        nc.vector.tensor_copy(out=b2[:], in_=b2_raw[:])
-
         half_rowsum = consts.tile([P, TILES], F32, name="half_rowsum")
         unread = consts.tile([P, GROUP, D], BF16, name="unread")
 
         fm, deep, grouped, codes, planes = {}, {}, {}, {}, {}
         h_bank, fm_bank, acc1, acc2, result = {}, {}, {}, {}, {}
+
+        def row_sum_on_vector(g, j):
+            nc.vector.tensor_scalar(
+                out=unread[:, j, :],
+                in0=x_in[g][:, j, :],
+                scalar1=0.5,
+                scalar2=0.0,
+                op0=ALU.mult,
+                op1=ALU.add,
+                accum_out=half_rowsum[:, g * GROUP + j : g * GROUP + j + 1],
+            )
 
         def row_sum(g, j):
             nc.scalar.activation(
@@ -132,11 +136,11 @@ def tile_deepfm_pa_t_kernel(
                 for u in range(2):
                     nc.tensor.transpose(h_bank[g, pair][:, j, u, :], words[:, u::2], identity[:])
 
-        def copy_h(g, pair):
+        def copy_h(g, pair, copy):
             if pair == 0:
                 grouped["h", g] = work.tile([P, GROUP * D], BF16, name="grouped_h", align_bytes=64)
             pairs = grouped["h", g][:].bitcast(F32).rearrange("p (j r u) -> p j r u", j=GROUP, u=2)
-            nc.scalar.copy(
+            copy(
                 out=pairs[:, 2 * pair : 2 * pair + 2, :, :],
                 in_=h_bank[g, pair][:].rearrange("p j u r -> p j r u"),
             )
@@ -204,34 +208,63 @@ def tile_deepfm_pa_t_kernel(
             return 0 <= g < GROUPS
 
         stack.enter_context(tc.manual_schedule())
-        for k in range(-2, GROUPS + 1):
-            if in_range(k + 2 + FIRST_LOADS):
-                load_group(k + 2 + FIRST_LOADS)
 
-            if in_range(k + 1):
-                quantise(("h", k + 1))
+        flip_h(0, 0)
+        flip_h(0, 1)
+        copy_h(0, 0, nc.scalar.copy)
+        copy_h(0, 1, nc.vector.tensor_copy)
+        nc.vector.tensor_copy(
+            out=w1_by_pass[:].bitcast(I32).rearrange("p (t m) -> p t m", t=PACK),
+            in_=w1_codes[:].bitcast(I32).rearrange("p (m t) -> p t m", t=PACK),
+        )
+        quantise(("h", 0))
+        nc.vector.tensor_copy(
+            out=w1_scales_by_pass[:].rearrange("p (t m) -> p t m", t=PACK),
+            in_=w1_scales[:].rearrange("p (m t) -> p t m", t=PACK),
+        )
+        nc.vector.tensor_scalar(out=half_b1[:], in0=b1_raw[:], scalar1=0.5, scalar2=None, op0=ALU.mult)
+        for g in range(VECTOR_SUM_GROUPS):
+            for j in range(GROUP):
+                row_sum_on_vector(g, j)
+                fm_product(g, j)
+        for t in range(PACK):
+            layer1(0, t)
+            leave_layer1(0, t)
+        for pair in range(2):
+            flip_h(1, pair)
+            copy_h(1, pair, nc.scalar.copy)
+        b2_bank = banks.tile([P, D], F32, name="acc2")
+        nc.tensor.matmul(b2_bank[:], ones[:], b2_row[:], start=True, stop=True)
+        nc.vector.tensor_copy(out=b2[:], in_=b2_bank[:])
+
+        for k in range(GROUPS + 1):
+            if in_range(k + FIRST_LOADS):
+                load_group(k + FIRST_LOADS)
+
             if in_range(k - 1):
                 quantise(("z", k - 1))
+            if in_range(k + 1):
+                quantise(("h", k + 1))
             for half in range(2):
                 pair = (2 * half, 2 * half + 1)
                 if in_range(k):
                     for j in pair:
                         flip_fm(k, j)
-                if in_range(k + 2) and half == 0:
-                    flip_h(k + 2, 0)
-                    flip_h(k + 2, 1)
-                    copy_h(k + 2, 0)
-                    copy_h(k + 2, 1)
-                if in_range(k + 1):
-                    for t in pair:
-                        layer1(k + 1, t)
+                if in_range(k + 2):
+                    flip_h(k + 2, half)
                 if in_range(k - 1):
                     for j in pair:
                         layer2(k - 1, j)
                 if in_range(k + 1):
-                    if half == 1:
+                    for t in pair:
+                        layer1(k + 1, t)
+                if in_range(k + 2):
+                    copy_h(k + 2, half, nc.scalar.copy)
+                if in_range(k + 1):
+                    if half == 0 and k + 1 >= VECTOR_SUM_GROUPS:
                         for j in range(GROUP):
                             row_sum(k + 1, j)
+                            fm_product(k + 1, j)
                     for t in pair:
                         leave_layer1(k + 1, t)
                 if in_range(k):
@@ -240,6 +273,3 @@ def tile_deepfm_pa_t_kernel(
                 if in_range(k - 1):
                     for j in pair:
                         leave_layer2(k - 1, j)
-                if in_range(k + 1) and half == 1:
-                    for j in range(GROUP):
-                        fm_product(k + 1, j)

@@ -18,6 +18,7 @@ D = 512
 PACK = 4
 TILES = B // P
 GROUP = 4
+RUN = 4
 GROUPS = TILES // GROUP
 FIRST_LOADS = 4
 INPUT_BUFS = 6
@@ -80,6 +81,11 @@ def tile_deepfm_pa_t_kernel(
 
         identity = consts.tile([P, P], F32, name="identity")
         make_identity(nc, identity[:])
+        row_order = consts.tile([P, P], F32, name="row_order")
+        nc.vector.tensor_copy(
+            out=row_order[:].rearrange("p (c i) -> p c i", i=RUN),
+            in_=identity[:].rearrange("p (i c) -> p c i", i=RUN),
+        )
         ones = consts.tile([P, P], BF16, name="ones")
         nc.gpsimd.memset(ones[:], 1.0)
         w1_by_pass = consts.tile([P, D * PACK], U8, name="w1_by_pass", align_bytes=64)
@@ -125,16 +131,16 @@ def tile_deepfm_pa_t_kernel(
             )
 
         def flip_fm(g, j):
-            fm_bank[g, j] = banks.tile([P, PACK, P], F32, name="fm_bank")
+            fm_bank[g, j] = banks.tile([P, P // RUN, PACK, RUN], F32, name="fm_bank")
             for t in range(PACK):
-                nc.tensor.transpose(fm_bank[g, j][:, t, :], fm[g][:, j, t, :], identity[:])
+                nc.tensor.transpose(fm_bank[g, j][:, :, t, :], fm[g][:, j, t, :], row_order[:])
 
         def flip_h(g, pair):
             h_bank[g, pair] = banks.tile([P, 2, 2, P], F32, name="h_bank")
             for j in range(2):
                 words = h_in[g][:, 2 * pair + j, :].bitcast(F32)
                 for u in range(2):
-                    nc.tensor.transpose(h_bank[g, pair][:, j, u, :], words[:, u::2], identity[:])
+                    nc.tensor.transpose(h_bank[g, pair][:, j, u, :], words[:, u::2], row_order[:])
 
         def copy_h(g, pair, copy):
             if pair == 0:
@@ -167,20 +173,24 @@ def tile_deepfm_pa_t_kernel(
 
         def leave_layer1(g, t):
             if t == 0:
-                deep[g] = work.tile([P, PACK, GROUP * P], F32, name="deep")
+                deep[g] = work.tile([P, GROUP, P // RUN, PACK, RUN], F32, name="deep", align_bytes=64)
             nc.scalar.activation(
-                out=deep[g][:, t, :], in_=acc1[g, t][:], func=ACT.Relu, scale=0.5, bias=half_b1[:, t : t + 1]
+                out=deep[g][:].rearrange("p j c t i -> p (j c) t i")[:, :, t, :],
+                in_=acc1[g, t][:].rearrange("p (c i) -> p c i", i=RUN),
+                func=ACT.Relu,
+                scale=0.5,
+                bias=half_b1[:, t : t + 1],
             )
 
         def make_z(g, j):
             if j == 0:
                 grouped["z", g] = work.tile([P, GROUP * D], BF16, name="grouped_z", align_bytes=64)
-            z = grouped["z", g][:].rearrange("p (j r t) -> p j r t", j=GROUP, t=PACK)
+            z = grouped["z", g][:].rearrange("p (j i m) -> p j m i", j=GROUP, i=RUN)
             nc.vector.scalar_tensor_tensor(
                 out=z[:, j, :, :],
-                in0=fm_bank[g, j][:].rearrange("p t r -> p r t"),
+                in0=fm_bank[g, j][:].rearrange("p c t i -> p (c t) i"),
                 scalar=0.0,
-                in1=deep[g][:, :, j * P : (j + 1) * P].rearrange("p t r -> p r t"),
+                in1=deep[g][:, j, :, :, :].rearrange("p c t i -> p (c t) i"),
                 op0=ALU.max,
                 op1=ALU.add,
             )

@@ -20,27 +20,32 @@ TILES = B // P
 GROUP = 4
 RUN = 4
 GROUPS = TILES // GROUP
-FIRST_LOADS = 4
+LOADS_AHEAD = 4
 INPUT_BUFS = 6
-VECTOR_SUM_GROUPS = 2
+WHOLE = slice(0, GROUP)
+HALVES = (slice(0, GROUP // 2), slice(GROUP // 2, GROUP))
 
 FLOPS = 2 * 2 * B * D * D
 
 
-def load_weight(nc, consts, words, scales, name):
-    codes = consts.tile([P, D * PACK], U8, name=name + "_codes", align_bytes=64)
+def load_codes(nc, consts, words, name):
+    codes = consts.tile([P, D * PACK], U8, name=name, align_bytes=64)
     nc.sync.dma_start(
         out=codes[:].bitcast(I32),
         in_=words.rearrange("g p n t -> (g p) (n t)").bitcast(I32),
     )
-    plane = consts.tile([P, D], U8, name=name + "_scales", align_bytes=64)
+    return codes
+
+
+def load_scales(nc, consts, scales, name):
+    plane = consts.tile([P, D], U8, name=name, align_bytes=64)
     nc.vector.memset(plane[:].bitcast(I32), 0)
     for quadrant in range(4):
         nc.sync.dma_start(
             out=plane[32 * quadrant : 32 * quadrant + 4, :].bitcast(I32),
             in_=scales[0, 4 * quadrant : 4 * quadrant + 4, :].bitcast(I32),
         )
-    return codes, plane
+    return plane
 
 
 def tile_deepfm_pa_t_kernel(
@@ -60,24 +65,35 @@ def tile_deepfm_pa_t_kernel(
 
         h_in, x_in = {}, {}
 
-        def load_group(g):
-            rows = slice(g * GROUP, (g + 1) * GROUP)
-            h_in[g] = inputs.tile([P, GROUP, D], BF16, name="h_in")
-            nc.sync.dma_start(out=h_in[g][:], in_=h_rows[:, rows, :])
-            x_in[g] = inputs.tile([P, GROUP, D], BF16, name="x_in")
-            nc.sync.dma_start(out=x_in[g][:], in_=x_rows[:, rows, :])
+        def load_rows(tiles, name, source, g, rows):
+            if g not in tiles:
+                tiles[g] = inputs.tile([P, GROUP, D], BF16, name=name)
+            nc.sync.dma_start(
+                out=tiles[g][:, rows, :], in_=source[:, g * GROUP + rows.start : g * GROUP + rows.stop, :]
+            )
 
-        load_group(0)
-        w1_codes, w1_scales = load_weight(nc, consts, w_last_words, w_last_scales, "w1")
+        def load_group(g):
+            load_rows(h_in, "h_in", h_rows, g, WHOLE)
+            load_rows(x_in, "x_in", x_rows, g, WHOLE)
+
+        load_rows(h_in, "h_in", h_rows, 0, HALVES[0])
+        w1_codes = load_codes(nc, consts, w_last_words, "w1_codes")
+        w1_scales = load_scales(nc, consts, w_last_scales, "w1_scales")
+        load_rows(x_in, "x_in", x_rows, 0, HALVES[0])
+        load_rows(h_in, "h_in", h_rows, 0, HALVES[1])
         b1_raw = consts.tile([P, PACK], BF16, name="b1_raw")
         nc.sync.dma_start(out=b1_raw[:], in_=b_last.rearrange("(p t) -> p t", t=PACK))
-        b2_row = consts.tile([P, D], BF16, name="b2_row")
-        nc.vector.memset(b2_row[:], 0.0)
-        nc.sync.dma_start(out=b2_row[:1, :], in_=b_out.rearrange("(o d) -> o d", o=1))
+        load_rows(x_in, "x_in", x_rows, 0, HALVES[1])
         load_group(1)
-        load_group(2)
-        w2_codes, w2_scales = load_weight(nc, consts, w_out_words, w_out_scales, "w2")
+        load_rows(h_in, "h_in", h_rows, 2, WHOLE)
+        b2_row = consts.tile([P, D], BF16, name="b2_row")
+        nc.gpsimd.memset(b2_row[:], 0.0)
+        nc.sync.dma_start(out=b2_row[:1, :], in_=b_out.rearrange("(o d) -> o d", o=1))
+        w2_codes = load_codes(nc, consts, w_out_words, "w2_codes")
+        w2_scales = load_scales(nc, consts, w_out_scales, "w2_scales")
+        load_rows(x_in, "x_in", x_rows, 2, WHOLE)
         load_group(3)
+        load_group(4)
 
         identity = consts.tile([P, P], F32, name="identity")
         make_identity(nc, identity[:])
@@ -151,32 +167,37 @@ def tile_deepfm_pa_t_kernel(
                 in_=h_bank[g, pair][:].rearrange("p j u r -> p j r u"),
             )
 
-        def quantise(key):
-            codes[key] = work.tile([P, GROUP * P], U32, name="codes_" + key[0], align_bytes=64)
-            planes[key] = work.tile([P, GROUP * P], U8, name="planes_" + key[0], align_bytes=64)
+        def quantise(key, rows):
+            if key not in codes:
+                codes[key] = work.tile([P, GROUP * P], U32, name="codes_" + key[0], align_bytes=64)
+                planes[key] = work.tile([P, GROUP * P], U8, name="planes_" + key[0], align_bytes=64)
+            cols = slice(rows.start * P, rows.stop * P)
             nc.vector.quantize_mx(
-                out=codes[key][:].bitcast(FP8X4), scales=planes[key][:], in_=grouped[key][:]
+                out=codes[key][:, cols].bitcast(FP8X4),
+                scales=planes[key][:, cols],
+                in_=grouped[key][:, PACK * cols.start : PACK * cols.stop],
             )
 
-        def layer1(g, t):
+        def layer1(g, t, rows):
             acc1[g, t] = banks.tile([P, GROUP * P], F32, name="acc1")
             cols = slice(t * P, (t + 1) * P)
+            moving = slice(rows.start * P, rows.stop * P)
             nc.tensor.matmul_mx(
-                out=acc1[g, t][:],
+                out=acc1[g, t][:, moving],
                 lhsT=w1_by_pass[:].bitcast(U32)[:, cols].bitcast(FP8X4),
                 lhsT_scale=w1_scales_by_pass[:, cols],
-                rhs=codes["h", g][:].bitcast(FP8X4),
-                rhs_scale=planes["h", g][:],
+                rhs=codes["h", g][:, moving].bitcast(FP8X4),
+                rhs_scale=planes["h", g][:, moving],
                 start=True,
                 stop=True,
             )
 
-        def leave_layer1(g, t):
-            if t == 0:
+        def leave_layer1(g, t, rows):
+            if g not in deep:
                 deep[g] = work.tile([P, GROUP, P // RUN, PACK, RUN], F32, name="deep", align_bytes=64)
             nc.scalar.activation(
-                out=deep[g][:].rearrange("p j c t i -> p (j c) t i")[:, :, t, :],
-                in_=acc1[g, t][:].rearrange("p (c i) -> p c i", i=RUN),
+                out=deep[g][:, rows, :, :, :].rearrange("p j c t i -> p (j c) t i")[:, :, t, :],
+                in_=acc1[g, t][:, rows.start * P : rows.stop * P].rearrange("p (c i) -> p c i", i=RUN),
                 func=ACT.Relu,
                 scale=0.5,
                 bias=half_b1[:, t : t + 1],
@@ -208,10 +229,14 @@ def tile_deepfm_pa_t_kernel(
                 stop=True,
             )
 
-        def leave_layer2(g, j):
-            if j == 0:
+        def leave_layer2(g, j, shared=False):
+            if g not in result:
                 result[g] = slack.tile([P, GROUP, D], F32, name="result")
-            nc.vector.tensor_tensor(out=result[g][:, j, :], in0=acc2[g, j][:], in1=b2[:], op=ALU.add)
+            if shared:
+                nc.scalar.copy(out=result[g][:, j, :], in_=acc2[g, j][:])
+                nc.gpsimd.tensor_tensor(out=result[g][:, j, :], in0=result[g][:, j, :], in1=b2[:], op=ALU.add)
+            else:
+                nc.vector.tensor_tensor(out=result[g][:, j, :], in0=acc2[g, j][:], in1=b2[:], op=ALU.add)
             nc.sync.dma_start(out=out_rows[:, g * GROUP + j, :], in_=result[g][:, j, :])
 
         def in_range(g):
@@ -222,64 +247,103 @@ def tile_deepfm_pa_t_kernel(
         flip_h(0, 0)
         flip_h(0, 1)
         copy_h(0, 0, nc.scalar.copy)
-        copy_h(0, 1, nc.vector.tensor_copy)
+        for j in (0, 1):
+            row_sum(0, j)
+            fm_product(0, j)
+        nc.scalar.mul(half_b1[:], b1_raw[:], 0.5)
         nc.vector.tensor_copy(
             out=w1_by_pass[:].bitcast(I32).rearrange("p (t m) -> p t m", t=PACK),
             in_=w1_codes[:].bitcast(I32).rearrange("p (m t) -> p t m", t=PACK),
         )
-        quantise(("h", 0))
         nc.vector.tensor_copy(
             out=w1_scales_by_pass[:].rearrange("p (t m) -> p t m", t=PACK),
             in_=w1_scales[:].rearrange("p (m t) -> p t m", t=PACK),
         )
-        nc.vector.tensor_scalar(out=half_b1[:], in0=b1_raw[:], scalar1=0.5, scalar2=None, op0=ALU.mult)
-        for g in range(VECTOR_SUM_GROUPS):
-            for j in range(GROUP):
-                row_sum_on_vector(g, j)
-                fm_product(g, j)
+        quantise(("h", 0), HALVES[0])
+        copy_h(0, 1, nc.vector.tensor_copy)
+        quantise(("h", 0), HALVES[1])
+        for j in (2, 3):
+            row_sum_on_vector(0, j)
+            fm_product(0, j)
         for t in range(PACK):
-            layer1(0, t)
-            leave_layer1(0, t)
-        for pair in range(2):
-            flip_h(1, pair)
-            copy_h(1, pair, nc.scalar.copy)
+            layer1(0, t, HALVES[0])
+            leave_layer1(0, t, HALVES[0])
+        flip_fm(0, 0)
+        flip_fm(0, 1)
+        for t in range(PACK):
+            layer1(0, t, HALVES[1])
+            leave_layer1(0, t, HALVES[1])
+        flip_h(1, 0)
+        flip_h(1, 1)
+        make_z(0, 0)
+        make_z(0, 1)
+        copy_h(1, 0, nc.vector.tensor_copy)
+        copy_h(1, 1, nc.scalar.copy)
+        for j in (0, 1):
+            row_sum_on_vector(1, j)
+            fm_product(1, j)
+        quantise(("h", 1), WHOLE)
+        flip_fm(0, 2)
+        flip_fm(0, 3)
+        flip_h(2, 0)
+        copy_h(2, 0, nc.scalar.copy)
+        flip_h(2, 1)
+        copy_h(2, 1, nc.scalar.copy)
+        for j in (2, 3):
+            row_sum_on_vector(1, j)
+            fm_product(1, j)
+        make_z(0, 2)
+        make_z(0, 3)
         b2_bank = banks.tile([P, D], F32, name="acc2")
         nc.tensor.matmul(b2_bank[:], ones[:], b2_row[:], start=True, stop=True)
+        for t in range(PACK):
+            layer1(1, t, WHOLE)
+            leave_layer1(1, t, WHOLE)
         nc.vector.tensor_copy(out=b2[:], in_=b2_bank[:])
 
-        for k in range(GROUPS + 1):
-            if in_range(k + FIRST_LOADS):
-                load_group(k + FIRST_LOADS)
+        for k in range(1, GROUPS - 1):
+            if in_range(k + LOADS_AHEAD):
+                load_group(k + LOADS_AHEAD)
 
-            if in_range(k - 1):
-                quantise(("z", k - 1))
-            if in_range(k + 1):
-                quantise(("h", k + 1))
+            quantise(("z", k - 1), WHOLE)
+            quantise(("h", k + 1), WHOLE)
             for half in range(2):
                 pair = (2 * half, 2 * half + 1)
-                if in_range(k):
-                    for j in pair:
-                        flip_fm(k, j)
+                for j in pair:
+                    flip_fm(k, j)
                 if in_range(k + 2):
                     flip_h(k + 2, half)
-                if in_range(k - 1):
-                    for j in pair:
-                        layer2(k - 1, j)
-                if in_range(k + 1):
-                    for t in pair:
-                        layer1(k + 1, t)
+                for j in pair:
+                    layer2(k - 1, j)
+                for t in pair:
+                    layer1(k + 1, t, WHOLE)
                 if in_range(k + 2):
                     copy_h(k + 2, half, nc.scalar.copy)
-                if in_range(k + 1):
-                    if half == 0 and k + 1 >= VECTOR_SUM_GROUPS:
-                        for j in range(GROUP):
-                            row_sum(k + 1, j)
-                            fm_product(k + 1, j)
-                    for t in pair:
-                        leave_layer1(k + 1, t)
-                if in_range(k):
-                    for j in pair:
-                        make_z(k, j)
-                if in_range(k - 1):
-                    for j in pair:
-                        leave_layer2(k - 1, j)
+                if half == 0:
+                    for j in range(GROUP):
+                        row_sum(k + 1, j)
+                        fm_product(k + 1, j)
+                for t in pair:
+                    leave_layer1(k + 1, t, WHOLE)
+                for j in pair:
+                    make_z(k, j)
+                for j in pair:
+                    leave_layer2(k - 1, j)
+
+        g = GROUPS - 1
+        quantise(("z", g - 1), WHOLE)
+        for half in range(2):
+            pair = (2 * half, 2 * half + 1)
+            for j in pair:
+                flip_fm(g, j)
+            for j in pair:
+                layer2(g - 1, j)
+            for j in pair:
+                make_z(g, j)
+            if half == 1:
+                quantise(("z", g), WHOLE)
+            for j in pair:
+                leave_layer2(g - 1, j, shared=j % 2 == 1)
+        for j in range(GROUP):
+            layer2(g, j)
+            leave_layer2(g, j, shared=j == 1)

@@ -20,8 +20,11 @@ TILES = B // P
 GROUP = 4
 RUN = 4
 GROUPS = TILES // GROUP
-LOADS_AHEAD = 4
-INPUT_BUFS = 6
+LOADS_AHEAD = 5
+INPUT_BUFS = 7
+DEEP_BUFS = 3
+FIRST_LOADS = 6
+VECTOR_SUMS = 9
 WHOLE = slice(0, GROUP)
 HALVES = (slice(0, GROUP // 2), slice(GROUP // 2, GROUP))
 
@@ -63,6 +66,8 @@ def tile_deepfm_pa_t_kernel(
         slack = stack.enter_context(tc.tile_pool(name="slack", bufs=3))
         banks = stack.enter_context(tc.psum_pool(name="banks", bufs=2))
 
+        ones = consts.tile([P, P], BF16, name="ones")
+        nc.vector.memset(ones[:], 1.0)
         h_in, x_in = {}, {}
 
         def load_rows(tiles, name, source, g, rows):
@@ -72,28 +77,32 @@ def tile_deepfm_pa_t_kernel(
                 out=tiles[g][:, rows, :], in_=source[:, g * GROUP + rows.start : g * GROUP + rows.stop, :]
             )
 
-        def load_group(g):
-            load_rows(h_in, "h_in", h_rows, g, WHOLE)
-            load_rows(x_in, "x_in", x_rows, g, WHOLE)
+        def load_h(g, rows=WHOLE):
+            load_rows(h_in, "h_in", h_rows, g, rows)
 
-        load_rows(h_in, "h_in", h_rows, 0, HALVES[0])
+        def load_x(g, rows=WHOLE):
+            load_rows(x_in, "x_in", x_rows, g, rows)
+
+        load_h(0, HALVES[0])
         w1_codes = load_codes(nc, consts, w_last_words, "w1_codes")
         w1_scales = load_scales(nc, consts, w_last_scales, "w1_scales")
-        load_rows(x_in, "x_in", x_rows, 0, HALVES[0])
-        load_rows(h_in, "h_in", h_rows, 0, HALVES[1])
+        load_x(0, HALVES[0])
+        load_h(0, HALVES[1])
         b1_raw = consts.tile([P, PACK], BF16, name="b1_raw")
         nc.sync.dma_start(out=b1_raw[:], in_=b_last.rearrange("(p t) -> p t", t=PACK))
-        load_rows(x_in, "x_in", x_rows, 0, HALVES[1])
-        load_group(1)
-        load_rows(h_in, "h_in", h_rows, 2, WHOLE)
+        load_x(0, HALVES[1])
+        load_h(1)
+        load_h(2)
+        load_x(1)
         b2_row = consts.tile([P, D], BF16, name="b2_row")
-        nc.gpsimd.memset(b2_row[:], 0.0)
+        nc.vector.memset(b2_row[:], 0.0)
         nc.sync.dma_start(out=b2_row[:1, :], in_=b_out.rearrange("(o d) -> o d", o=1))
         w2_codes = load_codes(nc, consts, w_out_words, "w2_codes")
         w2_scales = load_scales(nc, consts, w_out_scales, "w2_scales")
-        load_rows(x_in, "x_in", x_rows, 2, WHOLE)
-        load_group(3)
-        load_group(4)
+        for g in range(3, FIRST_LOADS):
+            load_h(g)
+            load_x(g - 1)
+        load_x(FIRST_LOADS - 1)
 
         identity = consts.tile([P, P], F32, name="identity")
         make_identity(nc, identity[:])
@@ -102,21 +111,20 @@ def tile_deepfm_pa_t_kernel(
             out=row_order[:].rearrange("p (c i) -> p c i", i=RUN),
             in_=identity[:].rearrange("p (i c) -> p c i", i=RUN),
         )
-        ones = consts.tile([P, P], BF16, name="ones")
-        nc.gpsimd.memset(ones[:], 1.0)
         w1_by_pass = consts.tile([P, D * PACK], U8, name="w1_by_pass", align_bytes=64)
         w1_scales_by_pass = consts.tile([P, D], U8, name="w1_scales_by_pass", align_bytes=64)
         half_b1 = consts.tile([P, PACK], F32, name="half_b1")
         b2 = consts.tile([P, D], F32, name="b2")
         half_rowsum = consts.tile([P, TILES], F32, name="half_rowsum")
-        unread = consts.tile([P, GROUP, D], BF16, name="unread")
+        unread_by_scalar = consts.tile([P, GROUP, D], BF16, name="unread_by_scalar")
+        unread_by_vector = consts.tile([P, GROUP, D], BF16, name="unread_by_vector")
 
         fm, deep, grouped, codes, planes = {}, {}, {}, {}, {}
         h_bank, fm_bank, acc1, acc2, result = {}, {}, {}, {}, {}
 
         def row_sum_on_vector(g, j):
             nc.vector.tensor_scalar(
-                out=unread[:, j, :],
+                out=unread_by_vector[:, j, :],
                 in0=x_in[g][:, j, :],
                 scalar1=0.5,
                 scalar2=0.0,
@@ -125,14 +133,21 @@ def tile_deepfm_pa_t_kernel(
                 accum_out=half_rowsum[:, g * GROUP + j : g * GROUP + j + 1],
             )
 
-        def row_sum(g, j):
+        def row_sum_on_scalar(g, j):
             nc.scalar.activation(
-                out=unread[:, j, :],
+                out=unread_by_scalar[:, j, :],
                 in_=x_in[g][:, j, :],
                 func=ACT.Copy,
                 scale=0.5,
                 accum_out=half_rowsum[:, g * GROUP + j : g * GROUP + j + 1],
             )
+
+        def row_product(g, j):
+            if 2 <= g * GROUP + j < VECTOR_SUMS:
+                row_sum_on_vector(g, j)
+            else:
+                row_sum_on_scalar(g, j)
+            fm_product(g, j)
 
         def fm_product(g, j):
             if j == 0:
@@ -194,7 +209,7 @@ def tile_deepfm_pa_t_kernel(
 
         def leave_layer1(g, t, rows):
             if g not in deep:
-                deep[g] = work.tile([P, GROUP, P // RUN, PACK, RUN], F32, name="deep", align_bytes=64)
+                deep[g] = work.tile([P, GROUP, P // RUN, PACK, RUN], F32, name="deep", align_bytes=64, bufs=DEEP_BUFS)
             nc.scalar.activation(
                 out=deep[g][:, rows, :, :, :].rearrange("p j c t i -> p (j c) t i")[:, :, t, :],
                 in_=acc1[g, t][:, rows.start * P : rows.stop * P].rearrange("p (c i) -> p c i", i=RUN),
@@ -245,12 +260,6 @@ def tile_deepfm_pa_t_kernel(
         stack.enter_context(tc.manual_schedule())
 
         flip_h(0, 0)
-        flip_h(0, 1)
-        copy_h(0, 0, nc.scalar.copy)
-        for j in (0, 1):
-            row_sum(0, j)
-            fm_product(0, j)
-        nc.scalar.mul(half_b1[:], b1_raw[:], 0.5)
         nc.vector.tensor_copy(
             out=w1_by_pass[:].bitcast(I32).rearrange("p (t m) -> p t m", t=PACK),
             in_=w1_codes[:].bitcast(I32).rearrange("p (m t) -> p t m", t=PACK),
@@ -259,91 +268,134 @@ def tile_deepfm_pa_t_kernel(
             out=w1_scales_by_pass[:].rearrange("p (t m) -> p t m", t=PACK),
             in_=w1_scales[:].rearrange("p (m t) -> p t m", t=PACK),
         )
+        copy_h(0, 0, nc.scalar.copy)
         quantise(("h", 0), HALVES[0])
+        flip_h(0, 1)
         copy_h(0, 1, nc.vector.tensor_copy)
         quantise(("h", 0), HALVES[1])
-        for j in (2, 3):
-            row_sum_on_vector(0, j)
-            fm_product(0, j)
+        row_product(0, 0)
+        row_product(0, 1)
+        nc.scalar.mul(half_b1[:], b1_raw[:], 0.5)
+        row_product(0, 2)
+        row_product(0, 3)
         for t in range(PACK):
             layer1(0, t, HALVES[0])
             leave_layer1(0, t, HALVES[0])
         flip_fm(0, 0)
         flip_fm(0, 1)
         for t in range(PACK):
+            if t == 2:
+                flip_h(1, 0)
             layer1(0, t, HALVES[1])
             leave_layer1(0, t, HALVES[1])
-        flip_h(1, 0)
-        flip_h(1, 1)
         make_z(0, 0)
         make_z(0, 1)
         copy_h(1, 0, nc.vector.tensor_copy)
-        copy_h(1, 1, nc.scalar.copy)
-        for j in (0, 1):
-            row_sum_on_vector(1, j)
-            fm_product(1, j)
-        quantise(("h", 1), WHOLE)
-        flip_fm(0, 2)
-        flip_fm(0, 3)
+        flip_h(1, 1)
         flip_h(2, 0)
         copy_h(2, 0, nc.scalar.copy)
-        flip_h(2, 1)
-        copy_h(2, 1, nc.scalar.copy)
-        for j in (2, 3):
-            row_sum_on_vector(1, j)
-            fm_product(1, j)
+        flip_fm(0, 2)
+        flip_fm(0, 3)
+        copy_h(1, 1, nc.vector.tensor_copy)
+        quantise(("h", 1), WHOLE)
         make_z(0, 2)
         make_z(0, 3)
-        b2_bank = banks.tile([P, D], F32, name="acc2")
-        nc.tensor.matmul(b2_bank[:], ones[:], b2_row[:], start=True, stop=True)
+        flip_h(2, 1)
+        copy_h(2, 1, nc.scalar.copy)
         for t in range(PACK):
             layer1(1, t, WHOLE)
             leave_layer1(1, t, WHOLE)
+        row_product(1, 0)
+        row_product(1, 1)
+        quantise(("h", 2), WHOLE)
+        row_product(1, 2)
+        row_product(1, 3)
+        b2_bank = banks.tile([P, D], F32, name="acc2")
+        nc.tensor.matmul(b2_bank[:], ones[:], b2_row[:], start=True, stop=True)
         nc.vector.tensor_copy(out=b2[:], in_=b2_bank[:])
+        flip_h(3, 0)
+        copy_h(3, 0, nc.scalar.copy)
+        flip_fm(1, 0)
+        flip_fm(1, 1)
+        flip_h(3, 1)
+        for t in (0, 1):
+            layer1(2, t, WHOLE)
+            leave_layer1(2, t, WHOLE)
+        copy_h(3, 1, nc.scalar.copy)
 
         for k in range(1, GROUPS - 1):
             if in_range(k + LOADS_AHEAD):
-                load_group(k + LOADS_AHEAD)
+                load_h(k + LOADS_AHEAD)
+                load_x(k + LOADS_AHEAD)
 
             quantise(("z", k - 1), WHOLE)
-            quantise(("h", k + 1), WHOLE)
-            for half in range(2):
-                pair = (2 * half, 2 * half + 1)
-                for j in pair:
-                    flip_fm(k, j)
-                if in_range(k + 2):
-                    flip_h(k + 2, half)
-                for j in pair:
-                    layer2(k - 1, j)
-                for t in pair:
-                    layer1(k + 1, t, WHOLE)
-                if in_range(k + 2):
-                    copy_h(k + 2, half, nc.scalar.copy)
-                if half == 0:
-                    for j in range(GROUP):
-                        row_sum(k + 1, j)
-                        fm_product(k + 1, j)
-                for t in pair:
-                    leave_layer1(k + 1, t, WHOLE)
-                for j in pair:
-                    make_z(k, j)
-                for j in pair:
-                    leave_layer2(k - 1, j)
+            layer2(k - 1, 0)
+            layer2(k - 1, 1)
+            layer1(k + 1, 2, WHOLE)
+            row_product(k + 1, 0)
+            leave_layer1(k + 1, 2, WHOLE)
+            make_z(k, 0)
+            make_z(k, 1)
+
+            flip_fm(k, 2)
+            flip_fm(k, 3)
+            if in_range(k + 3):
+                flip_h(k + 3, 0)
+            row_product(k + 1, 1)
+            if in_range(k + 3):
+                copy_h(k + 3, 0, nc.scalar.copy)
+            leave_layer2(k - 1, 0)
+            leave_layer2(k - 1, 1, shared=k == GROUPS - 2)
+
+            layer1(k + 1, 3, WHOLE)
+            layer2(k - 1, 2)
+            layer2(k - 1, 3)
+            row_product(k + 1, 2)
+            leave_layer1(k + 1, 3, WHOLE)
+            if in_range(k + 2):
+                quantise(("h", k + 2), WHOLE)
+            make_z(k, 2)
+            make_z(k, 3)
+
+            if in_range(k + 3):
+                flip_h(k + 3, 1)
+            flip_fm(k + 1, 0)
+            if in_range(k + 3):
+                copy_h(k + 3, 1, nc.scalar.copy)
+            row_product(k + 1, 3)
+            if in_range(k + 2):
+                layer1(k + 2, 0, WHOLE)
+                layer1(k + 2, 1, WHOLE)
+            flip_fm(k + 1, 1)
+            if in_range(k + 2):
+                leave_layer1(k + 2, 0, WHOLE)
+                leave_layer1(k + 2, 1, WHOLE)
+            leave_layer2(k - 1, 2)
+            leave_layer2(k - 1, 3)
 
         g = GROUPS - 1
         quantise(("z", g - 1), WHOLE)
-        for half in range(2):
-            pair = (2 * half, 2 * half + 1)
-            for j in pair:
-                flip_fm(g, j)
-            for j in pair:
-                layer2(g - 1, j)
-            for j in pair:
-                make_z(g, j)
-            if half == 1:
-                quantise(("z", g), WHOLE)
-            for j in pair:
-                leave_layer2(g - 1, j, shared=j % 2 == 1)
-        for j in range(GROUP):
-            layer2(g, j)
-            leave_layer2(g, j, shared=j == 1)
+        layer2(g - 1, 0)
+        layer2(g - 1, 1)
+        make_z(g, 0)
+        make_z(g, 1)
+        flip_fm(g, 2)
+        flip_fm(g, 3)
+        leave_layer2(g - 1, 0, shared=True)
+        leave_layer2(g - 1, 1)
+        layer2(g - 1, 2)
+        layer2(g - 1, 3)
+        make_z(g, 2)
+        quantise(("z", g), HALVES[0])
+        make_z(g, 3)
+        leave_layer2(g - 1, 2, shared=True)
+        leave_layer2(g - 1, 3)
+        quantise(("z", g), HALVES[1])
+        layer2(g, 0)
+        layer2(g, 1)
+        leave_layer2(g, 0)
+        leave_layer2(g, 1, shared=True)
+        layer2(g, 2)
+        layer2(g, 3)
+        leave_layer2(g, 2)
+        leave_layer2(g, 3)

@@ -22,9 +22,8 @@ RUN = 4
 GROUPS = TILES // GROUP
 LOADS_AHEAD = 5
 INPUT_BUFS = 7
-DEEP_BUFS = 3
 FIRST_LOADS = 6
-VECTOR_SUMS = 9
+VECTOR_SUMS = range(2, 8)
 WHOLE = slice(0, GROUP)
 HALVES = (slice(0, GROUP // 2), slice(GROUP // 2, GROUP))
 
@@ -91,12 +90,12 @@ def tile_deepfm_pa_t_kernel(
         b1_raw = consts.tile([P, PACK], BF16, name="b1_raw")
         nc.sync.dma_start(out=b1_raw[:], in_=b_last.rearrange("(p t) -> p t", t=PACK))
         load_x(0, HALVES[1])
-        load_h(1)
-        load_h(2)
-        load_x(1)
         b2_row = consts.tile([P, D], BF16, name="b2_row")
         nc.vector.memset(b2_row[:], 0.0)
         nc.sync.dma_start(out=b2_row[:1, :], in_=b_out.rearrange("(o d) -> o d", o=1))
+        load_h(1)
+        load_h(2)
+        load_x(1)
         w2_codes = load_codes(nc, consts, w_out_words, "w2_codes")
         w2_scales = load_scales(nc, consts, w_out_scales, "w2_scales")
         for g in range(3, FIRST_LOADS):
@@ -122,6 +121,9 @@ def tile_deepfm_pa_t_kernel(
         fm, deep, grouped, codes, planes = {}, {}, {}, {}, {}
         h_bank, fm_bank, acc1, acc2, result = {}, {}, {}, {}, {}
 
+        def pair_of(i):
+            return (i // 2 * 2, i // 2 * 2 + 1)
+
         def row_sum_on_vector(g, j):
             nc.vector.tensor_scalar(
                 out=unread_by_vector[:, j, :],
@@ -143,14 +145,14 @@ def tile_deepfm_pa_t_kernel(
             )
 
         def row_product(g, j):
-            if 2 <= g * GROUP + j < VECTOR_SUMS:
+            if g * GROUP + j in VECTOR_SUMS:
                 row_sum_on_vector(g, j)
             else:
                 row_sum_on_scalar(g, j)
             fm_product(g, j)
 
         def fm_product(g, j):
-            if j == 0:
+            if g not in fm:
                 fm[g] = work.tile([P, GROUP, PACK, P], F32, name="fm")
             nc.gpsimd.tensor_scalar(
                 out=fm[g][:, j, :, :],
@@ -162,7 +164,9 @@ def tile_deepfm_pa_t_kernel(
             )
 
         def flip_fm(g, j):
-            fm_bank[g, j] = banks.tile([P, P // RUN, PACK, RUN], F32, name="fm_bank")
+            if (g, j) not in fm_bank:
+                for n in pair_of(j):
+                    fm_bank[g, n] = banks.tile([P, P // RUN, PACK, RUN], F32, name="fm_bank")
             for t in range(PACK):
                 nc.tensor.transpose(fm_bank[g, j][:, :, t, :], fm[g][:, j, t, :], row_order[:])
 
@@ -174,7 +178,7 @@ def tile_deepfm_pa_t_kernel(
                     nc.tensor.transpose(h_bank[g, pair][:, j, u, :], words[:, u::2], row_order[:])
 
         def copy_h(g, pair, copy):
-            if pair == 0:
+            if ("h", g) not in grouped:
                 grouped["h", g] = work.tile([P, GROUP * D], BF16, name="grouped_h", align_bytes=64)
             pairs = grouped["h", g][:].bitcast(F32).rearrange("p (j r u) -> p j r u", j=GROUP, u=2)
             copy(
@@ -194,11 +198,13 @@ def tile_deepfm_pa_t_kernel(
             )
 
         def layer1(g, t, rows):
-            acc1[g, t] = banks.tile([P, GROUP * P], F32, name="acc1")
+            if (g, t, rows.start) not in acc1:
+                for n in pair_of(t):
+                    acc1[g, n, rows.start] = banks.tile([P, GROUP * P], F32, name="acc1")
             cols = slice(t * P, (t + 1) * P)
             moving = slice(rows.start * P, rows.stop * P)
             nc.tensor.matmul_mx(
-                out=acc1[g, t][:, moving],
+                out=acc1[g, t, rows.start][:, moving],
                 lhsT=w1_by_pass[:].bitcast(U32)[:, cols].bitcast(FP8X4),
                 lhsT_scale=w1_scales_by_pass[:, cols],
                 rhs=codes["h", g][:, moving].bitcast(FP8X4),
@@ -209,17 +215,17 @@ def tile_deepfm_pa_t_kernel(
 
         def leave_layer1(g, t, rows):
             if g not in deep:
-                deep[g] = work.tile([P, GROUP, P // RUN, PACK, RUN], F32, name="deep", align_bytes=64, bufs=DEEP_BUFS)
+                deep[g] = work.tile([P, GROUP, P // RUN, PACK, RUN], F32, name="deep", align_bytes=64)
             nc.scalar.activation(
                 out=deep[g][:, rows, :, :, :].rearrange("p j c t i -> p (j c) t i")[:, :, t, :],
-                in_=acc1[g, t][:, rows.start * P : rows.stop * P].rearrange("p (c i) -> p c i", i=RUN),
+                in_=acc1[g, t, rows.start][:, rows.start * P : rows.stop * P].rearrange("p (c i) -> p c i", i=RUN),
                 func=ACT.Relu,
                 scale=0.5,
                 bias=half_b1[:, t : t + 1],
             )
 
         def make_z(g, j):
-            if j == 0:
+            if ("z", g) not in grouped:
                 grouped["z", g] = work.tile([P, GROUP * D], BF16, name="grouped_z", align_bytes=64)
             z = grouped["z", g][:].rearrange("p (j i m) -> p j m i", j=GROUP, i=RUN)
             nc.vector.scalar_tensor_tensor(
@@ -232,7 +238,9 @@ def tile_deepfm_pa_t_kernel(
             )
 
         def layer2(g, j):
-            acc2[g, j] = banks.tile([P, D], F32, name="acc2")
+            if (g, j) not in acc2:
+                for n in pair_of(j):
+                    acc2[g, n] = banks.tile([P, D], F32, name="acc2")
             cols = slice(j * P, (j + 1) * P)
             nc.tensor.matmul_mx(
                 out=acc2[g, j][:],
@@ -252,7 +260,11 @@ def tile_deepfm_pa_t_kernel(
                 nc.gpsimd.tensor_tensor(out=result[g][:, j, :], in0=result[g][:, j, :], in1=b2[:], op=ALU.add)
             else:
                 nc.vector.tensor_tensor(out=result[g][:, j, :], in0=acc2[g, j][:], in1=b2[:], op=ALU.add)
-            nc.sync.dma_start(out=out_rows[:, g * GROUP + j, :], in_=result[g][:, j, :])
+
+        def store(g, rows):
+            nc.sync.dma_start(
+                out=out_rows[:, g * GROUP + rows.start : g * GROUP + rows.stop, :], in_=result[g][:, rows, :]
+            )
 
         def in_range(g):
             return 0 <= g < GROUPS
@@ -276,11 +288,11 @@ def tile_deepfm_pa_t_kernel(
         row_product(0, 0)
         row_product(0, 1)
         nc.scalar.mul(half_b1[:], b1_raw[:], 0.5)
-        row_product(0, 2)
-        row_product(0, 3)
         for t in range(PACK):
             layer1(0, t, HALVES[0])
             leave_layer1(0, t, HALVES[0])
+        row_product(0, 2)
+        row_product(0, 3)
         flip_fm(0, 0)
         flip_fm(0, 1)
         for t in range(PACK):
@@ -288,114 +300,110 @@ def tile_deepfm_pa_t_kernel(
                 flip_h(1, 0)
             layer1(0, t, HALVES[1])
             leave_layer1(0, t, HALVES[1])
-        make_z(0, 0)
+        b2_bank = banks.tile([P, D], F32, name="acc2")
+        nc.tensor.matmul(b2_bank[:], ones[:], b2_row[:], start=True, stop=True)
+        nc.scalar.copy(out=b2[:], in_=b2_bank[:])
         make_z(0, 1)
+        make_z(0, 0)
         copy_h(1, 0, nc.vector.tensor_copy)
         flip_h(1, 1)
         flip_h(2, 0)
         copy_h(2, 0, nc.scalar.copy)
-        flip_fm(0, 2)
         flip_fm(0, 3)
+        flip_fm(0, 2)
         copy_h(1, 1, nc.vector.tensor_copy)
         quantise(("h", 1), WHOLE)
+        row_product(1, 1)
+        row_product(1, 0)
         make_z(0, 2)
         make_z(0, 3)
         flip_h(2, 1)
         copy_h(2, 1, nc.scalar.copy)
-        for t in range(PACK):
-            layer1(1, t, WHOLE)
-            leave_layer1(1, t, WHOLE)
-        row_product(1, 0)
-        row_product(1, 1)
+        for pair in ((0, 1), (3, 2)):
+            for t in pair:
+                layer1(1, t, WHOLE)
+            for t in reversed(pair):
+                leave_layer1(1, t, WHOLE)
+        quantise(("z", 0), WHOLE)
         quantise(("h", 2), WHOLE)
         row_product(1, 2)
         row_product(1, 3)
-        b2_bank = banks.tile([P, D], F32, name="acc2")
-        nc.tensor.matmul(b2_bank[:], ones[:], b2_row[:], start=True, stop=True)
-        nc.vector.tensor_copy(out=b2[:], in_=b2_bank[:])
-        flip_h(3, 0)
-        copy_h(3, 0, nc.scalar.copy)
-        flip_fm(1, 0)
-        flip_fm(1, 1)
-        flip_h(3, 1)
-        for t in (0, 1):
-            layer1(2, t, WHOLE)
-            leave_layer1(2, t, WHOLE)
-        copy_h(3, 1, nc.scalar.copy)
 
         for k in range(1, GROUPS - 1):
             if in_range(k + LOADS_AHEAD):
                 load_h(k + LOADS_AHEAD)
                 load_x(k + LOADS_AHEAD)
 
-            quantise(("z", k - 1), WHOLE)
+            flip_fm(k, 0)
+            flip_fm(k, 1)
+            if in_range(k + 2):
+                flip_h(k + 2, 0)
             layer2(k - 1, 0)
             layer2(k - 1, 1)
-            layer1(k + 1, 2, WHOLE)
-            row_product(k + 1, 0)
-            leave_layer1(k + 1, 2, WHOLE)
-            make_z(k, 0)
+            layer1(k + 1, 0, WHOLE)
+            layer1(k + 1, 1, WHOLE)
+            for j in (1, 0, 2, 3):
+                row_product(k + 1, j)
+            leave_layer1(k + 1, 1, WHOLE)
+            leave_layer1(k + 1, 0, WHOLE)
             make_z(k, 1)
-
-            flip_fm(k, 2)
-            flip_fm(k, 3)
-            if in_range(k + 3):
-                flip_h(k + 3, 0)
-            row_product(k + 1, 1)
-            if in_range(k + 3):
-                copy_h(k + 3, 0, nc.scalar.copy)
+            make_z(k, 0)
+            leave_layer2(k - 1, 1)
             leave_layer2(k - 1, 0)
-            leave_layer2(k - 1, 1, shared=k == GROUPS - 2)
+            store(k - 1, HALVES[0])
 
-            layer1(k + 1, 3, WHOLE)
-            layer2(k - 1, 2)
-            layer2(k - 1, 3)
-            row_product(k + 1, 2)
-            leave_layer1(k + 1, 3, WHOLE)
+            flip_fm(k, 3)
+            flip_fm(k, 2)
             if in_range(k + 2):
-                quantise(("h", k + 2), WHOLE)
+                flip_h(k + 2, 1)
+            layer2(k - 1, 3)
+            layer2(k - 1, 2)
+            layer1(k + 1, 3, WHOLE)
+            layer1(k + 1, 2, WHOLE)
+            if in_range(k + 2):
+                copy_h(k + 2, 0, nc.scalar.copy)
+                copy_h(k + 2, 1, nc.scalar.copy)
+            leave_layer1(k + 1, 2, WHOLE)
+            leave_layer1(k + 1, 3, WHOLE)
             make_z(k, 2)
             make_z(k, 3)
-
-            if in_range(k + 3):
-                flip_h(k + 3, 1)
-            flip_fm(k + 1, 0)
-            if in_range(k + 3):
-                copy_h(k + 3, 1, nc.scalar.copy)
-            row_product(k + 1, 3)
-            if in_range(k + 2):
-                layer1(k + 2, 0, WHOLE)
-                layer1(k + 2, 1, WHOLE)
-            flip_fm(k + 1, 1)
-            if in_range(k + 2):
-                leave_layer1(k + 2, 0, WHOLE)
-                leave_layer1(k + 2, 1, WHOLE)
             leave_layer2(k - 1, 2)
             leave_layer2(k - 1, 3)
+            store(k - 1, HALVES[1])
+            quantise(("z", k), WHOLE)
+            if in_range(k + 2):
+                quantise(("h", k + 2), WHOLE)
 
         g = GROUPS - 1
-        quantise(("z", g - 1), WHOLE)
+        flip_fm(g, 0)
+        flip_fm(g, 1)
         layer2(g - 1, 0)
         layer2(g - 1, 1)
-        make_z(g, 0)
         make_z(g, 1)
-        flip_fm(g, 2)
+        make_z(g, 0)
+        leave_layer2(g - 1, 1, shared=True)
+        leave_layer2(g - 1, 0)
+        store(g - 1, HALVES[0])
         flip_fm(g, 3)
-        leave_layer2(g - 1, 0, shared=True)
-        leave_layer2(g - 1, 1)
-        layer2(g - 1, 2)
+        flip_fm(g, 2)
         layer2(g - 1, 3)
-        make_z(g, 2)
+        layer2(g - 1, 2)
         quantise(("z", g), HALVES[0])
+        make_z(g, 2)
         make_z(g, 3)
         leave_layer2(g - 1, 2, shared=True)
         leave_layer2(g - 1, 3)
-        quantise(("z", g), HALVES[1])
+        store(g - 1, HALVES[1])
         layer2(g, 0)
         layer2(g, 1)
         leave_layer2(g, 0)
+        store(g, slice(0, 1))
+        quantise(("z", g), HALVES[1])
         leave_layer2(g, 1, shared=True)
         layer2(g, 2)
         layer2(g, 3)
         leave_layer2(g, 2)
+        store(g, slice(2, 3))
+        store(g, slice(1, 2))
         leave_layer2(g, 3)
+        store(g, slice(3, 4))

@@ -23,7 +23,7 @@ GROUPS = TILES // GROUP
 LOADS_AHEAD = 5
 INPUT_BUFS = 7
 FIRST_LOADS = 6
-VECTOR_SUMS = range(2, 8)
+VECTOR_SUMS = range(1, 8)
 WHOLE = slice(0, GROUP)
 HALVES = (slice(0, GROUP // 2), slice(GROUP // 2, GROUP))
 
@@ -64,6 +64,8 @@ def tile_deepfm_pa_t_kernel(
         work = stack.enter_context(tc.tile_pool(name="work", bufs=2))
         slack = stack.enter_context(tc.tile_pool(name="slack", bufs=3))
         banks = stack.enter_context(tc.psum_pool(name="banks", bufs=2))
+
+        stack.enter_context(tc.manual_schedule())
 
         ones = consts.tile([P, P], BF16, name="ones")
         nc.vector.memset(ones[:], 1.0)
@@ -163,6 +165,15 @@ def tile_deepfm_pa_t_kernel(
                 op1=ALU.add,
             )
 
+        def fm_product_on_vector(g, j):
+            nc.vector.tensor_scalar(
+                out=fm[g][:, j, :, :],
+                in0=x_in[g][:, j, :].rearrange("p (q t) -> p t q", t=PACK),
+                scalar1=half_rowsum[:, g * GROUP + j : g * GROUP + j + 1],
+                scalar2=None,
+                op0=ALU.mult,
+            )
+
         def flip_fm(g, j):
             if (g, j) not in fm_bank:
                 for n in pair_of(j):
@@ -237,10 +248,10 @@ def tile_deepfm_pa_t_kernel(
                 op1=ALU.add,
             )
 
-        def layer2(g, j):
+        def layer2(g, j, bank="acc2"):
             if (g, j) not in acc2:
                 for n in pair_of(j):
-                    acc2[g, n] = banks.tile([P, D], F32, name="acc2")
+                    acc2[g, n] = banks.tile([P, D], F32, name=bank)
             cols = slice(j * P, (j + 1) * P)
             nc.tensor.matmul_mx(
                 out=acc2[g, j][:],
@@ -269,8 +280,6 @@ def tile_deepfm_pa_t_kernel(
         def in_range(g):
             return 0 <= g < GROUPS
 
-        stack.enter_context(tc.manual_schedule())
-
         flip_h(0, 0)
         nc.vector.tensor_copy(
             out=w1_by_pass[:].bitcast(I32).rearrange("p (t m) -> p t m", t=PACK),
@@ -282,15 +291,15 @@ def tile_deepfm_pa_t_kernel(
         )
         copy_h(0, 0, nc.scalar.copy)
         quantise(("h", 0), HALVES[0])
-        flip_h(0, 1)
-        copy_h(0, 1, nc.vector.tensor_copy)
-        quantise(("h", 0), HALVES[1])
         row_product(0, 0)
         row_product(0, 1)
         nc.scalar.mul(half_b1[:], b1_raw[:], 0.5)
+        flip_h(0, 1)
         for t in range(PACK):
             layer1(0, t, HALVES[0])
             leave_layer1(0, t, HALVES[0])
+        copy_h(0, 1, nc.vector.tensor_copy)
+        quantise(("h", 0), HALVES[1])
         row_product(0, 2)
         row_product(0, 3)
         flip_fm(0, 0)
@@ -326,8 +335,10 @@ def tile_deepfm_pa_t_kernel(
                 leave_layer1(1, t, WHOLE)
         quantise(("z", 0), WHOLE)
         quantise(("h", 2), WHOLE)
-        row_product(1, 2)
-        row_product(1, 3)
+        row_sum_on_vector(1, 2)
+        row_sum_on_vector(1, 3)
+        fm_product_on_vector(1, 2)
+        fm_product_on_vector(1, 3)
 
         for k in range(1, GROUPS - 1):
             if in_range(k + LOADS_AHEAD):
@@ -388,17 +399,17 @@ def tile_deepfm_pa_t_kernel(
         flip_fm(g, 2)
         layer2(g - 1, 3)
         layer2(g - 1, 2)
-        quantise(("z", g), HALVES[0])
         make_z(g, 2)
+        quantise(("z", g), HALVES[0])
         make_z(g, 3)
         leave_layer2(g - 1, 2, shared=True)
         leave_layer2(g - 1, 3)
         store(g - 1, HALVES[1])
-        layer2(g, 0)
-        layer2(g, 1)
+        layer2(g, 0, bank="acc1")
+        layer2(g, 1, bank="acc1")
+        quantise(("z", g), HALVES[1])
         leave_layer2(g, 0)
         store(g, slice(0, 1))
-        quantise(("z", g), HALVES[1])
         leave_layer2(g, 1, shared=True)
         layer2(g, 2)
         layer2(g, 3)

@@ -85,9 +85,9 @@ def tile_deepfm_pa_t_kernel(
             load_rows(x_in, "x_in", x_rows, g, rows)
 
         load_h(0, HALVES[0])
+        load_x(0, HALVES[0])
         w1_codes = load_codes(nc, consts, w_last_words, "w1_codes")
         w1_scales = load_scales(nc, consts, w_last_scales, "w1_scales")
-        load_x(0, HALVES[0])
         load_h(0, HALVES[1])
         b1_raw = consts.tile([P, PACK], BF16, name="b1_raw")
         nc.sync.dma_start(out=b1_raw[:], in_=b_last.rearrange("(p t) -> p t", t=PACK))
@@ -96,8 +96,8 @@ def tile_deepfm_pa_t_kernel(
         nc.vector.memset(b2_row[:], 0.0)
         nc.sync.dma_start(out=b2_row[:1, :], in_=b_out.rearrange("(o d) -> o d", o=1))
         load_h(1)
-        load_h(2)
         load_x(1)
+        load_h(2)
         w2_codes = load_codes(nc, consts, w_out_words, "w2_codes")
         w2_scales = load_scales(nc, consts, w_out_scales, "w2_scales")
         for g in range(3, FIRST_LOADS):
@@ -121,7 +121,7 @@ def tile_deepfm_pa_t_kernel(
         unread_by_vector = consts.tile([P, GROUP, D], BF16, name="unread_by_vector")
 
         fm, deep, grouped, codes, planes = {}, {}, {}, {}, {}
-        h_bank, fm_bank, acc1, acc2, result = {}, {}, {}, {}, {}
+        h_bank, fm_bank, acc1, half_acc1, acc2, result = {}, {}, {}, {}, {}, {}
 
         def pair_of(i):
             return (i // 2 * 2, i // 2 * 2 + 1)
@@ -211,7 +211,7 @@ def tile_deepfm_pa_t_kernel(
         def layer1(g, t, rows):
             if (g, t, rows.start) not in acc1:
                 for n in pair_of(t):
-                    acc1[g, n, rows.start] = banks.tile([P, GROUP * P], F32, name="acc1")
+                    acc1[g, n, rows.start] = banks.tile([P, GROUP * P], F32, name="acc1" if t < 2 or g != 1 else "acc2")
             cols = slice(t * P, (t + 1) * P)
             moving = slice(rows.start * P, rows.stop * P)
             nc.tensor.matmul_mx(
@@ -230,6 +230,32 @@ def tile_deepfm_pa_t_kernel(
             nc.scalar.activation(
                 out=deep[g][:, rows, :, :, :].rearrange("p j c t i -> p (j c) t i")[:, :, t, :],
                 in_=acc1[g, t, rows.start][:, rows.start * P : rows.stop * P].rearrange("p (c i) -> p c i", i=RUN),
+                func=ACT.Relu,
+                scale=0.5,
+                bias=half_b1[:, t : t + 1],
+            )
+
+        def layer1_half(g, t, half):
+            if (g, t // 2, half) not in half_acc1:
+                half_acc1[g, t // 2, half] = banks.tile([P, 2, GROUP // 2 * P], F32, name="acc1")
+            cols = slice(t * P, (t + 1) * P)
+            moving = slice(HALVES[half].start * P, HALVES[half].stop * P)
+            nc.tensor.matmul_mx(
+                out=half_acc1[g, t // 2, half][:, t % 2, :],
+                lhsT=w1_by_pass[:].bitcast(U32)[:, cols].bitcast(FP8X4),
+                lhsT_scale=w1_scales_by_pass[:, cols],
+                rhs=codes["h", g][:, moving].bitcast(FP8X4),
+                rhs_scale=planes["h", g][:, moving],
+                start=True,
+                stop=True,
+            )
+
+        def leave_layer1_half(g, t, half):
+            if g not in deep:
+                deep[g] = work.tile([P, GROUP, P // RUN, PACK, RUN], F32, name="deep", align_bytes=64)
+            nc.scalar.activation(
+                out=deep[g][:, HALVES[half], :, :, :].rearrange("p j c t i -> p (j c) t i")[:, :, t, :],
+                in_=half_acc1[g, t // 2, half][:, t % 2, :].rearrange("p (c i) -> p c i", i=RUN),
                 func=ACT.Relu,
                 scale=0.5,
                 bias=half_b1[:, t : t + 1],
@@ -281,64 +307,69 @@ def tile_deepfm_pa_t_kernel(
             return 0 <= g < GROUPS
 
         flip_h(0, 0)
+        row_sum_on_vector(0, 0)
+        fm_product(0, 0)
+        row_sum_on_vector(0, 1)
+        fm_product(0, 1)
+        copy_h(0, 0, nc.scalar.copy)
         nc.vector.tensor_copy(
             out=w1_by_pass[:].bitcast(I32).rearrange("p (t m) -> p t m", t=PACK),
             in_=w1_codes[:].bitcast(I32).rearrange("p (m t) -> p t m", t=PACK),
         )
+        quantise(("h", 0), HALVES[0])
         nc.vector.tensor_copy(
             out=w1_scales_by_pass[:].rearrange("p (t m) -> p t m", t=PACK),
             in_=w1_scales[:].rearrange("p (m t) -> p t m", t=PACK),
         )
-        copy_h(0, 0, nc.scalar.copy)
-        quantise(("h", 0), HALVES[0])
-        row_product(0, 0)
-        row_product(0, 1)
         nc.scalar.mul(half_b1[:], b1_raw[:], 0.5)
         flip_h(0, 1)
         for t in range(PACK):
-            layer1(0, t, HALVES[0])
-            leave_layer1(0, t, HALVES[0])
+            layer1_half(0, t, 0)
+        for t in range(PACK):
+            leave_layer1_half(0, t, 0)
         copy_h(0, 1, nc.vector.tensor_copy)
+        row_sum_on_vector(0, 2)
+        fm_product(0, 2)
         quantise(("h", 0), HALVES[1])
-        row_product(0, 2)
-        row_product(0, 3)
+        row_sum_on_vector(0, 3)
+        fm_product(0, 3)
         flip_fm(0, 0)
         flip_fm(0, 1)
-        for t in range(PACK):
-            if t == 2:
-                flip_h(1, 0)
-            layer1(0, t, HALVES[1])
-            leave_layer1(0, t, HALVES[1])
         b2_bank = banks.tile([P, D], F32, name="acc2")
         nc.tensor.matmul(b2_bank[:], ones[:], b2_row[:], start=True, stop=True)
         nc.scalar.copy(out=b2[:], in_=b2_bank[:])
-        make_z(0, 1)
         make_z(0, 0)
-        copy_h(1, 0, nc.vector.tensor_copy)
+        make_z(0, 1)
+        for t in range(PACK):
+            layer1_half(0, t, 1)
+        for t in range(PACK):
+            leave_layer1_half(0, t, 1)
+        flip_h(1, 0)
         flip_h(1, 1)
-        flip_h(2, 0)
-        copy_h(2, 0, nc.scalar.copy)
+        copy_h(1, 0, nc.vector.tensor_copy)
+        copy_h(1, 1, nc.scalar.copy)
+        quantise(("h", 1), WHOLE)
+        row_sum_on_scalar(1, 1)
+        fm_product(1, 1)
         flip_fm(0, 3)
         flip_fm(0, 2)
-        copy_h(1, 1, nc.vector.tensor_copy)
-        quantise(("h", 1), WHOLE)
-        row_product(1, 1)
-        row_product(1, 0)
-        make_z(0, 2)
-        make_z(0, 3)
+        flip_h(2, 0)
+        copy_h(2, 0, nc.scalar.copy)
         flip_h(2, 1)
         copy_h(2, 1, nc.scalar.copy)
-        for pair in ((0, 1), (3, 2)):
-            for t in pair:
-                layer1(1, t, WHOLE)
-            for t in reversed(pair):
-                leave_layer1(1, t, WHOLE)
+        for j in (0, 2):
+            row_sum_on_vector(1, j)
+            fm_product(1, j)
+        make_z(0, 2)
+        make_z(0, 3)
+        for t in range(PACK):
+            layer1(1, t, WHOLE)
+        for t in range(PACK):
+            leave_layer1(1, t, WHOLE)
         quantise(("z", 0), WHOLE)
         quantise(("h", 2), WHOLE)
-        row_sum_on_vector(1, 2)
-        row_sum_on_vector(1, 3)
-        fm_product_on_vector(1, 2)
-        fm_product_on_vector(1, 3)
+        row_sum_on_scalar(1, 3)
+        fm_product(1, 3)
 
         for k in range(1, GROUPS - 1):
             if in_range(k + LOADS_AHEAD):

@@ -18,7 +18,8 @@ D = 512
 PACK = 4
 TILES = B // P
 GROUP = 4
-RUN = 4
+PAIR = 2
+RUN = 2
 GROUPS = TILES // GROUP
 LOADS_AHEAD = 5
 INPUT_BUFS = 7
@@ -182,20 +183,17 @@ def tile_deepfm_pa_t_kernel(
                 nc.tensor.transpose(fm_bank[g, j][:, :, t, :], fm[g][:, j, t, :], row_order[:])
 
         def flip_h(g, pair):
-            h_bank[g, pair] = banks.tile([P, 2, 2, P], F32, name="h_bank")
+            h_bank[g, pair] = banks.tile([P, 2, P // RUN, PAIR, RUN], F32, name="h_bank")
             for j in range(2):
                 words = h_in[g][:, 2 * pair + j, :].bitcast(F32)
                 for u in range(2):
-                    nc.tensor.transpose(h_bank[g, pair][:, j, u, :], words[:, u::2], row_order[:])
+                    nc.tensor.transpose(h_bank[g, pair][:, u, :, j, :], words[:, u::2], row_order[:])
 
         def copy_h(g, pair, copy):
             if ("h", g) not in grouped:
                 grouped["h", g] = work.tile([P, GROUP * D], BF16, name="grouped_h", align_bytes=64)
-            pairs = grouped["h", g][:].bitcast(F32).rearrange("p (j r u) -> p j r u", j=GROUP, u=2)
-            copy(
-                out=pairs[:, 2 * pair : 2 * pair + 2, :, :],
-                in_=h_bank[g, pair][:].rearrange("p j u r -> p j r u"),
-            )
+            words = grouped["h", g][:].bitcast(F32).rearrange("p (b r u) -> p b r u", b=GROUP // PAIR, u=2)
+            copy(out=words[:, pair, :, :], in_=h_bank[g, pair][:].rearrange("p u c v i -> p (c v i) u"))
 
         def quantise(key, rows):
             if key not in codes:
@@ -226,10 +224,10 @@ def tile_deepfm_pa_t_kernel(
 
         def leave_layer1(g, t, rows):
             if g not in deep:
-                deep[g] = work.tile([P, GROUP, P // RUN, PACK, RUN], F32, name="deep", align_bytes=64)
+                deep[g] = work.tile([P, GROUP // PAIR, P // RUN, PACK, PAIR * RUN], F32, name="deep", align_bytes=64)
             nc.scalar.activation(
-                out=deep[g][:, rows, :, :, :].rearrange("p j c t i -> p (j c) t i")[:, :, t, :],
-                in_=acc1[g, t, rows.start][:, rows.start * P : rows.stop * P].rearrange("p (c i) -> p c i", i=RUN),
+                out=deep[g][:].rearrange("p b c t r -> p (b c) t r")[:, :, t, :],
+                in_=acc1[g, t, rows.start][:, rows.start * P : rows.stop * P].rearrange("p (c r) -> p c r", r=PAIR * RUN),
                 func=ACT.Relu,
                 scale=0.5,
                 bias=half_b1[:, t : t + 1],
@@ -252,10 +250,10 @@ def tile_deepfm_pa_t_kernel(
 
         def leave_layer1_half(g, t, half):
             if g not in deep:
-                deep[g] = work.tile([P, GROUP, P // RUN, PACK, RUN], F32, name="deep", align_bytes=64)
+                deep[g] = work.tile([P, GROUP // PAIR, P // RUN, PACK, PAIR * RUN], F32, name="deep", align_bytes=64)
             nc.scalar.activation(
-                out=deep[g][:, HALVES[half], :, :, :].rearrange("p j c t i -> p (j c) t i")[:, :, t, :],
-                in_=half_acc1[g, t // 2, half][:, t % 2, :].rearrange("p (c i) -> p c i", i=RUN),
+                out=deep[g][:, half, :, t, :],
+                in_=half_acc1[g, t // 2, half][:, t % 2, :].rearrange("p (c r) -> p c r", r=PAIR * RUN),
                 func=ACT.Relu,
                 scale=0.5,
                 bias=half_b1[:, t : t + 1],
@@ -269,7 +267,7 @@ def tile_deepfm_pa_t_kernel(
                 out=z[:, j, :, :],
                 in0=fm_bank[g, j][:].rearrange("p c t i -> p (c t) i"),
                 scalar=0.0,
-                in1=deep[g][:, j, :, :, :].rearrange("p c t i -> p (c t) i"),
+                in1=deep[g][:, j // PAIR, :, :, :].rearrange("p c t (v i) -> p v (c t) i", v=PAIR)[:, j % PAIR, :, :],
                 op0=ALU.max,
                 op1=ALU.add,
             )

@@ -408,7 +408,7 @@ def tile_deepfm_pa_t_kernel(
             make_z(k, 2)
             make_z(k, 3)
             leave_layer2(k - 1, 2)
-            leave_layer2(k - 1, 3)
+            leave_layer2(k - 1, 3, shared=not in_range(k + 2))
             store(k - 1, HALVES[1])
             quantise(("z", k), WHOLE)
             if in_range(k + 2):
@@ -417,8 +417,8 @@ def tile_deepfm_pa_t_kernel(
         g = GROUPS - 1
         flip_fm(g, 0)
         flip_fm(g, 1)
-        layer2(g - 1, 0)
-        layer2(g - 1, 1)
+        for j in range(GROUP):
+            layer2(g - 1, j, bank="acc1" if j < 2 else "acc2")
         make_z(g, 1)
         make_z(g, 0)
         leave_layer2(g - 1, 1, shared=True)
@@ -426,24 +426,17 @@ def tile_deepfm_pa_t_kernel(
         store(g - 1, HALVES[0])
         flip_fm(g, 3)
         flip_fm(g, 2)
-        layer2(g - 1, 3)
-        layer2(g - 1, 2)
+        make_z(g, 3)
         make_z(g, 2)
         quantise(("z", g), HALVES[0])
-        make_z(g, 3)
-        leave_layer2(g - 1, 2, shared=True)
-        leave_layer2(g - 1, 3)
-        store(g - 1, HALVES[1])
-        layer2(g, 0, bank="acc1")
-        layer2(g, 1, bank="acc1")
         quantise(("z", g), HALVES[1])
-        leave_layer2(g, 0)
-        store(g, slice(0, 1))
+        for j in (2, 3):
+            leave_layer2(g - 1, j)
+            store(g - 1, slice(j, j + 1))
+        for j in range(GROUP):
+            layer2(g, j, bank="acc1" if j < 2 else "h_bank")
         leave_layer2(g, 1, shared=True)
-        layer2(g, 2)
-        layer2(g, 3)
-        leave_layer2(g, 2)
-        store(g, slice(2, 3))
-        store(g, slice(1, 2))
-        leave_layer2(g, 3)
-        store(g, slice(3, 4))
+        for j in (0, 2, 3):
+            leave_layer2(g, j)
+        for j in (0, 2, 1, 3):
+            store(g, slice(j, j + 1))

@@ -63,7 +63,7 @@ def tile_deepfm_pa_t_kernel(
         consts = stack.enter_context(tc.tile_pool(name="consts", bufs=1))
         inputs = stack.enter_context(tc.tile_pool(name="inputs", bufs=INPUT_BUFS))
         work = stack.enter_context(tc.tile_pool(name="work", bufs=2))
-        slack = stack.enter_context(tc.tile_pool(name="slack", bufs=3))
+        slack = stack.enter_context(tc.tile_pool(name="slack", bufs=12))
         banks = stack.enter_context(tc.psum_pool(name="banks", bufs=2))
 
         stack.enter_context(tc.manual_schedule())
@@ -181,6 +181,13 @@ def tile_deepfm_pa_t_kernel(
                     fm_bank[g, n] = banks.tile([P, P // RUN, PACK, RUN], F32, name="fm_bank")
             for t in range(PACK):
                 nc.tensor.transpose(fm_bank[g, j][:, :, t, :], fm[g][:, j, t, :], row_order[:])
+
+        def keep_warm(g):
+            for n in pair_of(0):
+                fm_bank[g, n] = banks.tile([P, P // RUN, PACK, RUN], F32, name="fm_bank")
+            nc.tensor.matmul(
+                fm_bank[g, 0][:].rearrange("p c t i -> p (c t i)"), ones[:], b2_row[:], start=True, stop=True
+            )
 
         def flip_h(g, pair):
             h_bank[g, pair] = banks.tile([P, 2, P // RUN, PAIR, RUN], F32, name="h_bank")
@@ -374,6 +381,7 @@ def tile_deepfm_pa_t_kernel(
                 load_h(k + LOADS_AHEAD)
                 load_x(k + LOADS_AHEAD)
 
+            keep_warm(k)
             flip_fm(k, 0)
             flip_fm(k, 1)
             if in_range(k + 2):

@@ -26,6 +26,7 @@ INPUT_BUFS = 7
 FIRST_LOADS = 6
 VECTOR_SUMS = range(1, 8)
 WHOLE = slice(0, GROUP)
+LEFT, RIGHT = slice(0, D - 128), slice(D - 128, D)
 HALVES = (slice(0, GROUP // 2), slice(GROUP // 2, GROUP))
 
 FLOPS = 2 * 2 * B * D * D
@@ -294,14 +295,22 @@ def tile_deepfm_pa_t_kernel(
                 stop=True,
             )
 
-        def leave_layer2(g, j, shared=False):
+        def leave_layer2(g, j, shared=False, cols=slice(0, D)):
             if g not in result:
                 result[g] = slack.tile([P, GROUP, D], F32, name="result")
             if shared:
-                nc.scalar.copy(out=result[g][:, j, :], in_=acc2[g, j][:])
-                nc.gpsimd.tensor_tensor(out=result[g][:, j, :], in0=result[g][:, j, :], in1=b2[:], op=ALU.add)
+                copy_sum(g, j, cols)
+                add_b2(g, j, cols)
             else:
-                nc.vector.tensor_tensor(out=result[g][:, j, :], in0=acc2[g, j][:], in1=b2[:], op=ALU.add)
+                nc.vector.tensor_tensor(out=result[g][:, j, cols], in0=acc2[g, j][:, cols], in1=b2[:, cols], op=ALU.add)
+
+        def copy_sum(g, j, cols):
+            if g not in result:
+                result[g] = slack.tile([P, GROUP, D], F32, name="result")
+            nc.scalar.copy(out=result[g][:, j, cols], in_=acc2[g, j][:, cols])
+
+        def add_b2(g, j, cols):
+            nc.gpsimd.tensor_tensor(out=result[g][:, j, cols], in0=result[g][:, j, cols], in1=b2[:, cols], op=ALU.add)
 
         def store(g, rows):
             nc.sync.dma_start(
@@ -390,14 +399,18 @@ def tile_deepfm_pa_t_kernel(
             layer2(k - 1, 1)
             layer1(k + 1, 0, WHOLE)
             layer1(k + 1, 1, WHOLE)
-            for j in (1, 0, 2, 3):
+            for j in (1, 0):
                 row_product(k + 1, j)
+            copy_sum(k - 1, 0, RIGHT)
+            for j in (2, 3):
+                row_product(k + 1, j)
+            add_b2(k - 1, 0, RIGHT)
             leave_layer1(k + 1, 1, WHOLE)
             leave_layer1(k + 1, 0, WHOLE)
             make_z(k, 1)
             make_z(k, 0)
             leave_layer2(k - 1, 1)
-            leave_layer2(k - 1, 0)
+            leave_layer2(k - 1, 0, cols=LEFT)
             store(k - 1, HALVES[0])
 
             flip_fm(k, 3)

@@ -26,7 +26,8 @@ INPUT_BUFS = 7
 FIRST_LOADS = 6
 VECTOR_SUMS = range(1, 8)
 WHOLE = slice(0, GROUP)
-LEFT, RIGHT = slice(0, D - 128), slice(D - 128, D)
+SHARED_ROUNDS = range(3, GROUPS - 2)
+ALL, LEFT, RIGHT = slice(0, D), slice(0, D - 128), slice(D - 128, D)
 HALVES = (slice(0, GROUP // 2), slice(GROUP // 2, GROUP))
 
 FLOPS = 2 * 2 * B * D * D
@@ -214,10 +215,10 @@ def tile_deepfm_pa_t_kernel(
                 in_=grouped[key][:, PACK * cols.start : PACK * cols.stop],
             )
 
-        def layer1(g, t, rows):
+        def layer1(g, t, rows, bank="acc1"):
             if (g, t, rows.start) not in acc1:
                 for n in pair_of(t):
-                    acc1[g, n, rows.start] = banks.tile([P, GROUP * P], F32, name="acc1" if t < 2 or g != 1 else "acc2")
+                    acc1[g, n, rows.start] = banks.tile([P, GROUP * P], F32, name=bank)
             cols = slice(t * P, (t + 1) * P)
             moving = slice(rows.start * P, rows.stop * P)
             nc.tensor.matmul_mx(
@@ -295,7 +296,7 @@ def tile_deepfm_pa_t_kernel(
                 stop=True,
             )
 
-        def leave_layer2(g, j, shared=False, cols=slice(0, D)):
+        def leave_layer2(g, j, shared=False, cols=ALL):
             if g not in result:
                 result[g] = slack.tile([P, GROUP, D], F32, name="result")
             if shared:
@@ -377,7 +378,7 @@ def tile_deepfm_pa_t_kernel(
         make_z(0, 2)
         make_z(0, 3)
         for t in range(PACK):
-            layer1(1, t, WHOLE)
+            layer1(1, t, WHOLE, bank="acc1" if t < 2 else "acc2")
         for t in range(PACK):
             leave_layer1(1, t, WHOLE)
         quantise(("z", 0), WHOLE)
@@ -401,16 +402,18 @@ def tile_deepfm_pa_t_kernel(
             layer1(k + 1, 1, WHOLE)
             for j in (1, 0):
                 row_product(k + 1, j)
-            copy_sum(k - 1, 0, RIGHT)
+            if k in SHARED_ROUNDS:
+                copy_sum(k - 1, 0, RIGHT)
             for j in (2, 3):
                 row_product(k + 1, j)
-            add_b2(k - 1, 0, RIGHT)
+            if k in SHARED_ROUNDS:
+                add_b2(k - 1, 0, RIGHT)
             leave_layer1(k + 1, 1, WHOLE)
             leave_layer1(k + 1, 0, WHOLE)
             make_z(k, 1)
             make_z(k, 0)
             leave_layer2(k - 1, 1)
-            leave_layer2(k - 1, 0, cols=LEFT)
+            leave_layer2(k - 1, 0, cols=LEFT if k in SHARED_ROUNDS else ALL)
             store(k - 1, HALVES[0])
 
             flip_fm(k, 3)
@@ -419,8 +422,8 @@ def tile_deepfm_pa_t_kernel(
                 flip_h(k + 2, 1)
             layer2(k - 1, 3)
             layer2(k - 1, 2)
-            layer1(k + 1, 3, WHOLE)
-            layer1(k + 1, 2, WHOLE)
+            for t in (3, 2):
+                layer1(k + 1, t, WHOLE, bank="acc1" if in_range(k + 2) else "h_bank")
             if in_range(k + 2):
                 copy_h(k + 2, 0, nc.scalar.copy)
                 copy_h(k + 2, 1, nc.scalar.copy)

@@ -363,28 +363,29 @@ def tile_deepfm_pa_t_kernel(
         flip_h(1, 1)
         copy_h(1, 0, nc.vector.tensor_copy)
         copy_h(1, 1, nc.scalar.copy)
+        row_sum_on_vector(1, 0)
         quantise(("h", 1), WHOLE)
         row_sum_on_scalar(1, 1)
-        fm_product(1, 1)
+        for j in (1, 0):
+            fm_product(1, j)
         flip_fm(0, 3)
         flip_fm(0, 2)
         flip_h(2, 0)
         copy_h(2, 0, nc.scalar.copy)
         flip_h(2, 1)
         copy_h(2, 1, nc.scalar.copy)
-        for j in (0, 2):
-            row_sum_on_vector(1, j)
-            fm_product(1, j)
         make_z(0, 2)
         make_z(0, 3)
         for t in range(PACK):
             layer1(1, t, WHOLE, bank="acc1" if t < 2 else "acc2")
         for t in range(PACK):
             leave_layer1(1, t, WHOLE)
+        row_sum_on_vector(1, 2)
         quantise(("z", 0), WHOLE)
         quantise(("h", 2), WHOLE)
-        row_sum_on_scalar(1, 3)
-        fm_product(1, 3)
+        row_sum_on_vector(1, 3)
+        for j in (3, 2):
+            fm_product(1, j)
 
         for k in range(1, GROUPS - 1):
             if in_range(k + LOADS_AHEAD):

from contextlib import ExitStack

import concourse.mybir as mybir
from concourse.masks import make_identity

F32 = mybir.dt.float32
BF16 = mybir.dt.bfloat16
I32 = mybir.dt.int32
U32 = mybir.dt.uint32
U8 = mybir.dt.uint8
FP8X4 = mybir.dt.float8_e4m3fn_x4
ALU = mybir.AluOpType
ACT = mybir.ActivationFunctionType

P = 128
B = 8192
D = 512
PACK = 4
TILES = B // P
GROUP = 4
PAIR = 2
RUN = 2
GROUPS = TILES // GROUP
LOADS_AHEAD = 5
INPUT_BUFS = 7
FIRST_LOADS = 6
VECTOR_SUMS = range(1, 8)
WHOLE = slice(0, GROUP)
SHARED_ROUNDS = range(3, GROUPS - 2)
ALL, LEFT, RIGHT = slice(0, D), slice(0, D - 128), slice(D - 128, D)
HALVES = (slice(0, GROUP // 2), slice(GROUP // 2, GROUP))

FLOPS = 2 * 2 * B * D * D


def load_codes(nc, consts, words, name):
    codes = consts.tile([P, D * PACK], U8, name=name, align_bytes=64)
    nc.sync.dma_start(
        out=codes[:].bitcast(I32),
        in_=words.rearrange("g p n t -> (g p) (n t)").bitcast(I32),
    )
    return codes


def load_scales(nc, consts, scales, name):
    plane = consts.tile([P, D], U8, name=name, align_bytes=64)
    nc.vector.memset(plane[:].bitcast(I32), 0)
    for quadrant in range(4):
        nc.sync.dma_start(
            out=plane[32 * quadrant : 32 * quadrant + 4, :].bitcast(I32),
            in_=scales[0, 4 * quadrant : 4 * quadrant + 4, :].bitcast(I32),
        )
    return plane


def tile_deepfm_pa_t_kernel(
    tc, h_prev, x, w_last_words, w_last_scales, b_last, w_out_words, w_out_scales, b_out, out
):
    nc = tc.nc
    h_rows = h_prev.rearrange("(p t) d -> p t d", t=TILES)
    x_rows = x.rearrange("(p t) d -> p t d", t=TILES)
    out_rows = out.rearrange("(p t) d -> p t d", t=TILES)

    with ExitStack() as stack:
        consts = stack.enter_context(tc.tile_pool(name="consts", bufs=1))
        inputs = stack.enter_context(tc.tile_pool(name="inputs", bufs=INPUT_BUFS))
        work = stack.enter_context(tc.tile_pool(name="work", bufs=2))
        slack = stack.enter_context(tc.tile_pool(name="slack", bufs=12))
        banks = stack.enter_context(tc.psum_pool(name="banks", bufs=2))

        stack.enter_context(tc.manual_schedule())

        ones = consts.tile([P, P], BF16, name="ones")
        nc.vector.memset(ones[:], 1.0)
        h_in, x_in = {}, {}

        def load_rows(tiles, name, source, g, rows):
            if g not in tiles:
                tiles[g] = inputs.tile([P, GROUP, D], BF16, name=name)
            nc.sync.dma_start(
                out=tiles[g][:, rows, :], in_=source[:, g * GROUP + rows.start : g * GROUP + rows.stop, :]
            )

        def load_h(g, rows=WHOLE):
            load_rows(h_in, "h_in", h_rows, g, rows)

        def load_x(g, rows=WHOLE):
            load_rows(x_in, "x_in", x_rows, g, rows)

        load_h(0, HALVES[0])
        load_x(0, HALVES[0])
        w1_codes = load_codes(nc, consts, w_last_words, "w1_codes")
        w1_scales = load_scales(nc, consts, w_last_scales, "w1_scales")
        load_h(0, HALVES[1])
        b1_raw = consts.tile([P, PACK], BF16, name="b1_raw")
        nc.sync.dma_start(out=b1_raw[:], in_=b_last.rearrange("(p t) -> p t", t=PACK))
        load_x(0, HALVES[1])
        b2_row = consts.tile([P, D], BF16, name="b2_row")
        nc.vector.memset(b2_row[:], 0.0)
        nc.sync.dma_start(out=b2_row[:1, :], in_=b_out.rearrange("(o d) -> o d", o=1))
        load_h(1)
        load_x(1)
        load_h(2)
        w2_codes = load_codes(nc, consts, w_out_words, "w2_codes")
        w2_scales = load_scales(nc, consts, w_out_scales, "w2_scales")
        for g in range(3, FIRST_LOADS):
            load_h(g)
            load_x(g - 1)
        load_x(FIRST_LOADS - 1)

        identity = consts.tile([P, P], F32, name="identity")
        make_identity(nc, identity[:])
        row_order = consts.tile([P, P], F32, name="row_order")
        nc.vector.tensor_copy(
            out=row_order[:].rearrange("p (c i) -> p c i", i=RUN),
            in_=identity[:].rearrange("p (i c) -> p c i", i=RUN),
        )
        w1_by_pass = consts.tile([P, D * PACK], U8, name="w1_by_pass", align_bytes=64)
        w1_scales_by_pass = consts.tile([P, D], U8, name="w1_scales_by_pass", align_bytes=64)
        half_b1 = consts.tile([P, PACK], F32, name="half_b1")
        b2 = consts.tile([P, D], F32, name="b2")
        half_rowsum = consts.tile([P, TILES], F32, name="half_rowsum")
        unread_by_scalar = consts.tile([P, GROUP, D], BF16, name="unread_by_scalar")
        unread_by_vector = consts.tile([P, GROUP, D], BF16, name="unread_by_vector")

        fm, deep, grouped, codes, planes = {}, {}, {}, {}, {}
        h_bank, fm_bank, acc1, half_acc1, acc2, result = {}, {}, {}, {}, {}, {}

        def pair_of(i):
            return (i // 2 * 2, i // 2 * 2 + 1)

        def row_sum_on_vector(g, j):
            nc.vector.tensor_scalar(
                out=unread_by_vector[:, j, :],
                in0=x_in[g][:, j, :],
                scalar1=0.5,
                scalar2=0.0,
                op0=ALU.mult,
                op1=ALU.add,
                accum_out=half_rowsum[:, g * GROUP + j : g * GROUP + j + 1],
            )

        def row_sum_on_scalar(g, j):
            nc.scalar.activation(
                out=unread_by_scalar[:, j, :],
                in_=x_in[g][:, j, :],
                func=ACT.Copy,
                scale=0.5,
                accum_out=half_rowsum[:, g * GROUP + j : g * GROUP + j + 1],
            )

        def row_product(g, j):
            if g * GROUP + j in VECTOR_SUMS:
                row_sum_on_vector(g, j)
            else:
                row_sum_on_scalar(g, j)
            fm_product(g, j)

        def fm_product(g, j):
            if g not in fm:
                fm[g] = work.tile([P, GROUP, PACK, P], F32, name="fm")
            nc.gpsimd.tensor_scalar(
                out=fm[g][:, j, :, :],
                in0=x_in[g][:, j, :].rearrange("p (q t) -> p t q", t=PACK),
                scalar1=half_rowsum[:, g * GROUP + j : g * GROUP + j + 1],
                scalar2=0.0,
                op0=ALU.mult,
                op1=ALU.add,
            )

        def fm_product_on_vector(g, j):
            nc.vector.tensor_scalar(
                out=fm[g][:, j, :, :],
                in0=x_in[g][:, j, :].rearrange("p (q t) -> p t q", t=PACK),
                scalar1=half_rowsum[:, g * GROUP + j : g * GROUP + j + 1],
                scalar2=None,
                op0=ALU.mult,
            )

        def flip_fm(g, j):
            if (g, j) not in fm_bank:
                for n in pair_of(j):
                    fm_bank[g, n] = banks.tile([P, P // RUN, PACK, RUN], F32, name="fm_bank")
            for t in range(PACK):
                nc.tensor.transpose(fm_bank[g, j][:, :, t, :], fm[g][:, j, t, :], row_order[:])

        def keep_warm(g):
            for n in pair_of(0):
                fm_bank[g, n] = banks.tile([P, P // RUN, PACK, RUN], F32, name="fm_bank")
            nc.tensor.matmul(
                fm_bank[g, 0][:].rearrange("p c t i -> p (c t i)"), ones[:], b2_row[:], start=True, stop=True
            )

        def flip_h(g, pair):
            h_bank[g, pair] = banks.tile([P, 2, P // RUN, PAIR, RUN], F32, name="h_bank")
            for j in range(2):
                words = h_in[g][:, 2 * pair + j, :].bitcast(F32)
                for u in range(2):
                    nc.tensor.transpose(h_bank[g, pair][:, u, :, j, :], words[:, u::2], row_order[:])

        def copy_h(g, pair, copy):
            if ("h", g) not in grouped:
                grouped["h", g] = work.tile([P, GROUP * D], BF16, name="grouped_h", align_bytes=64)
            words = grouped["h", g][:].bitcast(F32).rearrange("p (b r u) -> p b r u", b=GROUP // PAIR, u=2)
            copy(out=words[:, pair, :, :], in_=h_bank[g, pair][:].rearrange("p u c v i -> p (c v i) u"))

        def quantise(key, rows):
            if key not in codes:
                codes[key] = work.tile([P, GROUP * P], U32, name="codes_" + key[0], align_bytes=64)
                planes[key] = work.tile([P, GROUP * P], U8, name="planes_" + key[0], align_bytes=64)
            cols = slice(rows.start * P, rows.stop * P)
            nc.vector.quantize_mx(
                out=codes[key][:, cols].bitcast(FP8X4),
                scales=planes[key][:, cols],
                in_=grouped[key][:, PACK * cols.start : PACK * cols.stop],
            )

        def layer1(g, t, rows, bank="acc1"):
            if (g, t, rows.start) not in acc1:
                for n in pair_of(t):
                    acc1[g, n, rows.start] = banks.tile([P, GROUP * P], F32, name=bank)
            cols = slice(t * P, (t + 1) * P)
            moving = slice(rows.start * P, rows.stop * P)
            nc.tensor.matmul_mx(
                out=acc1[g, t, rows.start][:, moving],
                lhsT=w1_by_pass[:].bitcast(U32)[:, cols].bitcast(FP8X4),
                lhsT_scale=w1_scales_by_pass[:, cols],
                rhs=codes["h", g][:, moving].bitcast(FP8X4),
                rhs_scale=planes["h", g][:, moving],
                start=True,
                stop=True,
            )

        def leave_layer1(g, t, rows):
            if g not in deep:
                deep[g] = work.tile([P, GROUP // PAIR, P // RUN, PACK, PAIR * RUN], F32, name="deep", align_bytes=64)
            nc.scalar.activation(
                out=deep[g][:].rearrange("p b c t r -> p (b c) t r")[:, :, t, :],
                in_=acc1[g, t, rows.start][:, rows.start * P : rows.stop * P].rearrange("p (c r) -> p c r", r=PAIR * RUN),
                func=ACT.Relu,
                scale=0.5,
                bias=half_b1[:, t : t + 1],
            )

        def layer1_half(g, t, half):
            if (g, t // 2, half) not in half_acc1:
                half_acc1[g, t // 2, half] = banks.tile([P, 2, GROUP // 2 * P], F32, name="acc1")
            cols = slice(t * P, (t + 1) * P)
            moving = slice(HALVES[half].start * P, HALVES[half].stop * P)
            nc.tensor.matmul_mx(
                out=half_acc1[g, t // 2, half][:, t % 2, :],
                lhsT=w1_by_pass[:].bitcast(U32)[:, cols].bitcast(FP8X4),
                lhsT_scale=w1_scales_by_pass[:, cols],
                rhs=codes["h", g][:, moving].bitcast(FP8X4),
                rhs_scale=planes["h", g][:, moving],
                start=True,
                stop=True,
            )

        def leave_layer1_half(g, t, half):
            if g not in deep:
                deep[g] = work.tile([P, GROUP // PAIR, P // RUN, PACK, PAIR * RUN], F32, name="deep", align_bytes=64)
            nc.scalar.activation(
                out=deep[g][:, half, :, t, :],
                in_=half_acc1[g, t // 2, half][:, t % 2, :].rearrange("p (c r) -> p c r", r=PAIR * RUN),
                func=ACT.Relu,
                scale=0.5,
                bias=half_b1[:, t : t + 1],
            )

        def make_z(g, j):
            if ("z", g) not in grouped:
                grouped["z", g] = work.tile([P, GROUP * D], BF16, name="grouped_z", align_bytes=64)
            z = grouped["z", g][:].rearrange("p (j i m) -> p j m i", j=GROUP, i=RUN)
            nc.vector.scalar_tensor_tensor(
                out=z[:, j, :, :],
                in0=fm_bank[g, j][:].rearrange("p c t i -> p (c t) i"),
                scalar=0.0,
                in1=deep[g][:, j // PAIR, :, :, :].rearrange("p c t (v i) -> p v (c t) i", v=PAIR)[:, j % PAIR, :, :],
                op0=ALU.max,
                op1=ALU.add,
            )

        def layer2(g, j, bank="acc2"):
            if (g, j) not in acc2:
                for n in pair_of(j):
                    acc2[g, n] = banks.tile([P, D], F32, name=bank)
            cols = slice(j * P, (j + 1) * P)
            nc.tensor.matmul_mx(
                out=acc2[g, j][:],
                lhsT=codes["z", g][:, cols].bitcast(FP8X4),
                lhsT_scale=planes["z", g][:, cols],
                rhs=w2_codes[:].bitcast(FP8X4),
                rhs_scale=w2_scales[:],
                start=True,
                stop=True,
            )

        def leave_layer2(g, j, shared=False, cols=ALL):
            if g not in result:
                result[g] = slack.tile([P, GROUP, D], F32, name="result")
            if shared:
                copy_sum(g, j, cols)
                add_b2(g, j, cols)
            else:
                nc.vector.tensor_tensor(out=result[g][:, j, cols], in0=acc2[g, j][:, cols], in1=b2[:, cols], op=ALU.add)

        def copy_sum(g, j, cols):
            if g not in result:
                result[g] = slack.tile([P, GROUP, D], F32, name="result")
            nc.scalar.copy(out=result[g][:, j, cols], in_=acc2[g, j][:, cols])

        def add_b2(g, j, cols):
            nc.gpsimd.tensor_tensor(out=result[g][:, j, cols], in0=result[g][:, j, cols], in1=b2[:, cols], op=ALU.add)

        def store(g, rows):
            nc.sync.dma_start(
                out=out_rows[:, g * GROUP + rows.start : g * GROUP + rows.stop, :], in_=result[g][:, rows, :]
            )

        def in_range(g):
            return 0 <= g < GROUPS

        flip_h(0, 0)
        row_sum_on_vector(0, 0)
        fm_product(0, 0)
        row_sum_on_vector(0, 1)
        fm_product(0, 1)
        copy_h(0, 0, nc.scalar.copy)
        nc.vector.tensor_copy(
            out=w1_by_pass[:].bitcast(I32).rearrange("p (t m) -> p t m", t=PACK),
            in_=w1_codes[:].bitcast(I32).rearrange("p (m t) -> p t m", t=PACK),
        )
        quantise(("h", 0), HALVES[0])
        nc.vector.tensor_copy(
            out=w1_scales_by_pass[:].rearrange("p (t m) -> p t m", t=PACK),
            in_=w1_scales[:].rearrange("p (m t) -> p t m", t=PACK),
        )
        nc.scalar.mul(half_b1[:], b1_raw[:], 0.5)
        flip_h(0, 1)
        for t in range(PACK):
            layer1_half(0, t, 0)
        for t in range(PACK):
            leave_layer1_half(0, t, 0)
        copy_h(0, 1, nc.vector.tensor_copy)
        row_sum_on_vector(0, 2)
        fm_product(0, 2)
        quantise(("h", 0), HALVES[1])
        row_sum_on_vector(0, 3)
        fm_product(0, 3)
        flip_fm(0, 0)
        flip_fm(0, 1)
        b2_bank = banks.tile([P, D], F32, name="acc2")
        nc.tensor.matmul(b2_bank[:], ones[:], b2_row[:], start=True, stop=True)
        nc.scalar.copy(out=b2[:], in_=b2_bank[:])
        make_z(0, 0)
        make_z(0, 1)
        for t in range(PACK):
            layer1_half(0, t, 1)
        for t in range(PACK):
            leave_layer1_half(0, t, 1)
        flip_h(1, 0)
        flip_h(1, 1)
        copy_h(1, 0, nc.vector.tensor_copy)
        copy_h(1, 1, nc.scalar.copy)
        row_sum_on_vector(1, 0)
        quantise(("h", 1), WHOLE)
        row_sum_on_scalar(1, 1)
        for j in (1, 0):
            fm_product(1, j)
        flip_fm(0, 3)
        flip_fm(0, 2)
        flip_h(2, 0)
        copy_h(2, 0, nc.scalar.copy)
        flip_h(2, 1)
        copy_h(2, 1, nc.scalar.copy)
        make_z(0, 2)
        make_z(0, 3)
        for t in range(PACK):
            layer1(1, t, WHOLE, bank="acc1" if t < 2 else "acc2")
        for t in range(PACK):
            leave_layer1(1, t, WHOLE)
        row_sum_on_vector(1, 2)
        quantise(("z", 0), WHOLE)
        quantise(("h", 2), WHOLE)
        row_sum_on_vector(1, 3)
        for j in (3, 2):
            fm_product(1, j)

        for k in range(1, GROUPS - 1):
            if in_range(k + LOADS_AHEAD):
                load_h(k + LOADS_AHEAD)
                load_x(k + LOADS_AHEAD)

            keep_warm(k)
            flip_fm(k, 0)
            flip_fm(k, 1)
            if in_range(k + 2):
                flip_h(k + 2, 0)
            layer2(k - 1, 0)
            layer2(k - 1, 1)
            layer1(k + 1, 0, WHOLE)
            layer1(k + 1, 1, WHOLE)
            for j in (1, 0):
                row_product(k + 1, j)
            if k in SHARED_ROUNDS:
                copy_sum(k - 1, 0, RIGHT)
            for j in (2, 3):
                row_product(k + 1, j)
            if k in SHARED_ROUNDS:
                add_b2(k - 1, 0, RIGHT)
            leave_layer1(k + 1, 1, WHOLE)
            leave_layer1(k + 1, 0, WHOLE)
            make_z(k, 1)
            make_z(k, 0)
            leave_layer2(k - 1, 1)
            leave_layer2(k - 1, 0, cols=LEFT if k in SHARED_ROUNDS else ALL)
            store(k - 1, HALVES[0])

            flip_fm(k, 3)
            flip_fm(k, 2)
            if in_range(k + 2):
                flip_h(k + 2, 1)
            layer2(k - 1, 3)
            layer2(k - 1, 2)
            for t in (3, 2):
                layer1(k + 1, t, WHOLE, bank="acc1" if in_range(k + 2) else "h_bank")
            if in_range(k + 2):
                copy_h(k + 2, 0, nc.scalar.copy)
                copy_h(k + 2, 1, nc.scalar.copy)
            leave_layer1(k + 1, 2, WHOLE)
            leave_layer1(k + 1, 3, WHOLE)
            make_z(k, 2)
            make_z(k, 3)
            leave_layer2(k - 1, 2)
            leave_layer2(k - 1, 3, shared=not in_range(k + 2))
            store(k - 1, HALVES[1])
            quantise(("z", k), WHOLE)
            if in_range(k + 2):
                quantise(("h", k + 2), WHOLE)

        g = GROUPS - 1
        flip_fm(g, 0)
        flip_fm(g, 1)
        for j in range(GROUP):
            layer2(g - 1, j, bank="acc1" if j < 2 else "acc2")
        make_z(g, 1)
        make_z(g, 0)
        leave_layer2(g - 1, 1, shared=True)
        leave_layer2(g - 1, 0)
        store(g - 1, HALVES[0])
        flip_fm(g, 3)
        flip_fm(g, 2)
        make_z(g, 3)
        make_z(g, 2)
        quantise(("z", g), HALVES[0])
        quantise(("z", g), HALVES[1])
        for j in (2, 3):
            leave_layer2(g - 1, j)
            store(g - 1, slice(j, j + 1))
        for j in range(GROUP):
            layer2(g, j, bank="acc1" if j < 2 else "h_bank")
        leave_layer2(g, 1, shared=True)
        for j in (0, 2, 3):
            leave_layer2(g, j)
        for j in (0, 2, 1, 3):
            store(g, slice(j, j + 1))
